import numpy as np
import ml_dtypes


def mxq(x, axis, fmt="e4m3"):
    dtype, down = {"e4m3": (ml_dtypes.float8_e4m3fn, 7), "e5m2": (ml_dtypes.float8_e5m2, 14)}[fmt]
    v = np.moveaxis(np.asarray(x, np.float32).astype(ml_dtypes.bfloat16).astype(np.float64), axis, -1)
    blocks = v.reshape(v.shape[:-1] + (-1, 32))
    amax = np.abs(blocks).max(-1, keepdims=True)
    byte = np.maximum(np.where(amax > 0, np.frexp(amax)[1] - 1 + 127, 0) - down, 1)
    scale = np.exp2(byte - 127.0)
    codes = (blocks / scale).astype(np.float32).astype(dtype).astype(np.float64)
    return np.moveaxis((codes * scale).reshape(v.shape), -1, axis)


WIDE = False


def mx_kscale(k):
    if not WIDE:
        return np.ones(k)
    levels = np.array([10, -10, 5, -5, 0])
    a = np.random.permutation(np.resize(levels, k // 512 * 4)).reshape(k // 512, 4)
    idx = np.arange(k)
    return np.exp2(a[idx // 512, idx % 128 // 32])


BF16 = ml_dtypes.bfloat16


def bf(x):
    return np.asarray(x, np.float32).astype(BF16)


def f64(x):
    return np.asarray(x).astype(np.float64)


E2M1 = np.array([0.0, 0.5, 1.0, 1.5, 2.0, 3.0, 4.0, 6.0, -0.0, -0.5, -1.0, -1.5, -2.0, -3.0, -4.0, -6.0])


def pack_weight(w, fmt):
    k, n = w.shape
    w = f64(bf(w)).reshape(k // 32, 32, n)
    amax = np.abs(w).max(1)
    if fmt == "e4m3":
        byte = np.frexp(amax)[1] - 1 + 127 - 7
    else:
        mant, ex = np.frexp(amax / 6.0)
        byte = np.where(mant > 0.5, ex, ex - 1) + 127
    byte = np.clip(np.where(amax > 0, byte, 1), 1, 254)
    scaled = (w * np.exp2(127.0 - byte)[:, None, :]).reshape(k, n).astype(np.float32)
    by_word = np.ascontiguousarray(scaled.reshape(k // 512, 128, 4, n).transpose(0, 1, 3, 2))
    if fmt == "e4m3":
        words = by_word.astype(ml_dtypes.float8_e4m3fn).view(np.uint8)
    else:
        c = by_word.astype(ml_dtypes.float4_e2m1fn).view(np.uint8) & 0xF
        words = c[..., 0::2] | (c[..., 1::2] << 4)
    return np.ascontiguousarray(words), np.ascontiguousarray(byte.astype(np.uint8).reshape(k // 512, 16, n))


def unpack_weight(words, scales, fmt):
    g, p, n, _ = words.shape
    if fmt == "e4m3":
        vals = np.ascontiguousarray(words).view(ml_dtypes.float8_e4m3fn).astype(np.float64)
    else:
        nib = np.empty((g, p, n, 4), np.uint8)
        nib[..., 0::2] = words & 0xF
        nib[..., 1::2] = words >> 4
        vals = E2M1[nib]
    vals = vals * np.repeat(np.exp2(scales.astype(np.float64) - 127.0), 8, axis=1)[..., None]
    return vals.transpose(0, 1, 3, 2).reshape(g * 512, n)


B, HI, WI, F, D, NH, C = 1, 64, 64, 1024, 256, 3, 16
N = HI * WI
EPS = 1e-12
FMT = "e4m3"


def l2norm_rows(a):
    n = np.sqrt(np.sum(a * a, axis=1, keepdims=True))
    return a / np.maximum(n, EPS)


def setup_inputs():
    s = mx_kscale(F)

    def w():
        full = np.random.standard_normal((D, F)) / np.sqrt(F) / s[None, :]
        return pack_weight(np.ascontiguousarray(full.T), FMT)

    def b():
        return bf(np.random.standard_normal(D) * 0.2)

    x = bf(np.random.standard_normal((B, F, HI, WI)) * s[None, :, None, None])
    W1_words, W1_scales = w()
    b1 = b()
    W2_words, W2_scales = w()
    b2 = b()
    W3_words, W3_scales = w()
    b3 = b()
    return {"x": x,
            "W1_words": W1_words, "W1_scales": W1_scales, "b1": b1,
            "W2_words": W2_words, "W2_scales": W2_scales, "b2": b2,
            "W3_words": W3_words, "W3_scales": W3_scales, "b3": b3}


def reference(x, W1_words, W1_scales, b1, W2_words, W2_scales, b2, W3_words, W3_scales, b3):
    xq = mxq(f64(x).reshape(F, N).T, 1, "e4m3")
    heads = [l2norm_rows((xq @ unpack_weight(words, scales, FMT)) + f64(b))
             for words, scales, b in ((W1_words, W1_scales, b1), (W2_words, W2_scales, b2), (W3_words, W3_scales, b3))]
    return np.stack(heads)

@@ -1,0 +1,223 @@
+from contextlib import ExitStack
+
+import concourse.mybir as mybir
+
+F32 = mybir.dt.float32
+BF16 = mybir.dt.bfloat16
+I32 = mybir.dt.int32
+U32 = mybir.dt.uint32
+U8 = mybir.dt.uint8
+FP8X4 = mybir.dt.float8_e4m3fn_x4
+ACT = mybir.ActivationFunctionType
+ALU = mybir.AluOpType
+
+P = 128
+PACK = 4
+K_PASS = P * PACK
+FEATURES = 1024
+PASSES = FEATURES // K_PASS
+PIXELS = 64 * 64
+HEADS = 3
+D = 256
+TILES = 4
+CHUNK = TILES * P
+CHUNKS = PIXELS // CHUNK
+PAIR = 2
+PAIRS = TILES // PAIR
+EPS = 1e-12
+VECTOR_UNITS = 1
+HEAD_CHUNKS = 2
+
+FLOPS = 2 * PIXELS * FEATURES * HEADS * D
+
+
+def tile_gat_pa_t_kernel(
+    tc, x, W1_words, W1_scales, b1, W2_words, W2_scales, b2, W3_words, W3_scales, b3, out
+):
+    nc = tc.nc
+    xf = x.rearrange("b f i j -> (b f) (i j)")
+    units = [(k, e) for e in range(PAIR) for k in (0, 1)] + [(2, e) for e in range(PAIR)]
+
+    with ExitStack() as ctx:
+        const = ctx.enter_context(tc.tile_pool(name="const", bufs=1))
+        raw_pool = ctx.enter_context(tc.tile_pool(name="raw", bufs=CHUNKS * PASSES))
+        grouped_pool = ctx.enter_context(tc.tile_pool(name="grouped", bufs=4))
+        mx_pool = ctx.enter_context(tc.tile_pool(name="mx", bufs=3))
+        h_pool = ctx.enter_context(tc.tile_pool(name="h", bufs=4))
+        small = ctx.enter_context(tc.tile_pool(name="small", bufs=4))
+        psum12 = ctx.enter_context(tc.psum_pool(name="psum12", bufs=2 * PAIR))
+        psum3 = ctx.enter_context(tc.psum_pool(name="psum3", bufs=2))
+
+        raw, grouped, x_codes, x_scales = {}, {}, {}, {}
+        acc12, acc3, h, sums, rinv = {}, {}, {}, {}, {}
+
+        def load(c):
+            for g in range(PASSES):
+                raw[c, g] = raw_pool.tile([P, PACK, CHUNK], BF16, name="raw", tag="raw")
+                rows = xf[g * K_PASS : (g + 1) * K_PASS, c * CHUNK : (c + 1) * CHUNK]
+                nc.sync.dma_start(out=raw[c, g][:], in_=rows.rearrange("(p j) w -> p j w", j=PACK))
+
+        def regroup(copy, c, g):
+            grouped[c, g] = grouped_pool.tile(
+                [P, TILES, P, PACK], BF16, name="grouped", tag="grouped", align_bytes=64
+            )
+            copy(
+                out=grouped[c, g][:].rearrange("p i m j -> p m j i"),
+                in_=raw[c, g][:].rearrange("p j (m i) -> p m j i", i=TILES),
+            )
+
+        def quantise(c, g):
+            if g == 0:
+                x_codes[c] = mx_pool.tile([P, PASSES, CHUNK], U32, name="x_codes", tag="x_codes", align_bytes=64)
+                x_scales[c] = mx_pool.tile([P, PASSES, CHUNK], U8, name="x_scales", tag="x_scales", align_bytes=64)
+            nc.vector.quantize_mx(
+                out=x_codes[c][:, g, :].bitcast(FP8X4),
+                scales=x_scales[c][:, g, :],
+                in_=grouped[c, g][:].rearrange("p i m j -> p (i m j)"),
+            )
+
+        def project(c, pair):
+            acc3[c, pair] = psum3.tile([P, PAIR, D], F32, name="acc3", tag="acc3")
+            for e in range(PAIR):
+                acc12[c, pair, e] = psum12.tile([P, 2, D], F32, name="acc12", tag="acc12")
+                first = (pair * PAIR + e) * P
+                for g in range(PASSES):
+                    for columns, acc in (
+                        (slice(0, 2 * D), acc12[c, pair, e][:].rearrange("p k d -> p (k d)")),
+                        (slice(2 * D, 3 * D), acc3[c, pair][:, e, :]),
+                    ):
+                        nc.tensor.matmul_mx(
+                            out=acc,
+                            lhsT=x_codes[c][:, g, first : first + P].bitcast(FP8X4),
+                            lhsT_scale=x_scales[c][:, g, first : first + P],
+                            rhs=w_codes[:, g, columns].bitcast(FP8X4),
+                            rhs_scale=w_scales[:, g, columns],
+                            start=(g == 0),
+                            stop=(g == PASSES - 1),
+                        )
+
+        def add_bias(c, pair):
+            if pair == 0:
+                h[c] = h_pool.tile([P, HEADS, TILES, D], F32, name="h", tag="h")
+            for e in range(PAIR):
+                nc.vector.tensor_tensor(
+                    out=h[c][:, 0:2, pair * PAIR + e, :], in0=acc12[c, pair, e][:], in1=bias[:, 0:2, :], op=ALU.add
+                )
+            nc.vector.tensor_tensor(
+                out=h[c][:, 2, pair * PAIR : (pair + 1) * PAIR, :],
+                in0=acc3[c, pair][:],
+                in1=bias[:, 2:3, :].to_broadcast([P, PAIR, D]),
+                op=ALU.add,
+            )
+
+        def square_sums(c, pair):
+            sums[c, pair] = small.tile([P, len(units)], F32, name="sums", tag="sums")
+            for u, (k, e) in enumerate(units):
+                nc.scalar.activation(
+                    out=discard[:],
+                    in_=h[c][:, k, pair * PAIR + e, :],
+                    func=ACT.Square,
+                    accum_out=sums[c, pair][:, u : u + 1],
+                )
+
+        def inverse_norms(c, pair):
+            floored = small.tile([P, len(units)], F32, name="floored", tag="floored")
+            inverse = small.tile([P, len(units)], F32, name="inverse", tag="inverse")
+            rinv[c, pair] = small.tile([P, len(units)], F32, name="rinv", tag="rinv")
+            nc.vector.tensor_scalar_max(out=floored[:], in0=sums[c, pair][:], scalar1=EPS * EPS)
+            nc.vector.reciprocal(out=inverse[:], in_=floored[:])
+            nc.scalar.sqrt(out=rinv[c, pair][:], in_=inverse[:])
+
+        def scale_on_scalar(c, pair):
+            for u, (k, e) in enumerate(units):
+                if u >= VECTOR_UNITS:
+                    rows = h[c][:, k, pair * PAIR + e, :]
+                    nc.scalar.activation(out=rows, in_=rows, func=ACT.Copy, scale=rinv[c, pair][:, u : u + 1])
+
+        def scale_on_vector(c, pair):
+            for u, (k, e) in enumerate(units):
+                if u < VECTOR_UNITS:
+                    rows = h[c][:, k, pair * PAIR + e, :]
+                    nc.vector.tensor_scalar_mul(out=rows, in0=rows, scalar1=rinv[c, pair][:, u : u + 1])
+
+        def store(c):
+            nc.sync.dma_start(
+                out=out[:, c * CHUNK : (c + 1) * CHUNK, :].rearrange("k (p i) d -> p k (i d)", i=TILES),
+                in_=h[c][:].rearrange("p k i d -> p k (i d)"),
+            )
+
+        w_codes = const.tile([P, PASSES, HEADS * D], U32, name="w_codes", align_bytes=64)
+        w_scales = const.tile([P, PASSES, HEADS * D], U8, name="w_scales", align_bytes=64)
+        bias_rows = const.tile([P, HEADS, D], BF16, name="bias_rows")
+        ones = const.tile([P, P], BF16, name="ones")
+        bias = const.tile([P, HEADS, D], F32, name="bias")
+        discard = const.tile([P, D], F32, name="discard")
+        warm = const.tile([P, 1], F32, name="warm")
+
+        nc.vector.memset(w_scales[:].bitcast(I32), 0)
+        nc.vector.memset(bias_rows[:], 0.0)
+        nc.vector.memset(ones[:], 1.0)
+        nc.vector.memset(warm[:], 1.0)
+        nc.scalar.sqrt(out=warm[:], in_=warm[:])
+
+        load(0)
+        for k, (words, scales) in enumerate(((W1_words, W1_scales), (W2_words, W2_scales), (W3_words, W3_scales))):
+            columns = slice(k * D, (k + 1) * D)
+            for quadrant in range(4):
+                nc.sync.dma_start(
+                    out=w_scales[32 * quadrant : 32 * quadrant + 4, :, columns].bitcast(I32),
+                    in_=scales[:, 4 * quadrant : 4 * quadrant + 4, :].rearrange("g q n -> q g n").bitcast(I32),
+                )
+            nc.sync.dma_start(
+                out=w_codes[:, :, columns].bitcast(I32),
+                in_=words.rearrange("g p n t -> p g (n t)").bitcast(I32),
+            )
+        for k, b in enumerate((b1, b2, b3)):
+            nc.scalar.dma_start(out=bias_rows[0:1, k, :], in_=b.rearrange("(o d) -> o d", o=1))
+        for c in range(1, CHUNKS):
+            load(c)
+
+        def pass1_copy(c):
+            return nc.scalar.copy if c < HEAD_CHUNKS else nc.vector.tensor_copy
+
+        regroup(nc.vector.tensor_copy, 0, 0)
+        regroup(pass1_copy(0), 0, 1)
+        quantise(0, 0)
+        quantise(0, 1)
+
+        spread12 = psum12.tile([P, 2, D], F32, name="spread12", tag="acc12")
+        spread3 = psum3.tile([P, PAIR, D], F32, name="spread3", tag="acc3")
+        nc.tensor.matmul(
+            out=spread12[:].rearrange("p k d -> p (k d)"),
+            lhsT=ones[:],
+            rhs=bias_rows[:, 0:2, :].rearrange("p k d -> p (k d)"),
+            start=True,
+            stop=True,
+        )
+        nc.tensor.matmul(out=spread3[:, 0, :], lhsT=ones[:], rhs=bias_rows[:, 2, :], start=True, stop=True)
+        nc.scalar.copy(out=bias[:, 0:2, :], in_=spread12[:])
+        nc.scalar.copy(out=bias[:, 2, :], in_=spread3[:, 0, :])
+
+        for c in range(CHUNKS + 1):
+            if c + 1 < CHUNKS:
+                regroup(nc.vector.tensor_copy, c + 1, 0)
+            if c > 0:
+                inverse_norms(c - 1, 1)
+                scale_on_vector(c - 1, 0)
+                scale_on_scalar(c - 1, 1)
+            if c + 1 < CHUNKS:
+                regroup(pass1_copy(c + 1), c + 1, 1)
+                quantise(c + 1, 0)
+            if c > 0:
+                scale_on_vector(c - 1, 1)
+                store(c - 1)
+            if c + 1 < CHUNKS:
+                quantise(c + 1, 1)
+            if c < CHUNKS:
+                for pair in range(PAIRS):
+                    project(c, pair)
+                for pair in range(PAIRS):
+                    add_bias(c, pair)
+                    square_sums(c, pair)
+                inverse_norms(c, 0)
+                scale_on_scalar(c, 0)

@@ -47,6 +47,7 @@ def tile_gat_pa_t_kernel(
         small = ctx.enter_context(tc.tile_pool(name="small", bufs=4))
         psum12 = ctx.enter_context(tc.psum_pool(name="psum12", bufs=2 * PAIR))
         psum3 = ctx.enter_context(tc.psum_pool(name="psum3", bufs=2))
+        ctx.enter_context(tc.manual_schedule())
 
         raw, grouped, x_codes, x_scales = {}, {}, {}, {}
         acc12, acc3, h, sums, rinv = {}, {}, {}, {}, {}

@@ -26,7 +26,8 @@ PAIR = 2
 PAIRS = TILES // PAIR
 EPS = 1e-12
 VECTOR_UNITS = 1
-HEAD_CHUNKS = 2
+VECTOR_UNITS_LAST = 3
+SCALAR_QUEUE_CHUNKS = 3
 
 FLOPS = 2 * PIXELS * FEATURES * HEADS * D
 
@@ -52,19 +53,17 @@ def tile_gat_pa_t_kernel(
         raw, grouped, x_codes, x_scales = {}, {}, {}, {}
         acc12, acc3, h, sums, rinv = {}, {}, {}, {}, {}
 
-        def load(c):
+        def load(queue, c):
             for g in range(PASSES):
                 raw[c, g] = raw_pool.tile([P, PACK, CHUNK], BF16, name="raw", tag="raw")
                 rows = xf[g * K_PASS : (g + 1) * K_PASS, c * CHUNK : (c + 1) * CHUNK]
-                nc.sync.dma_start(out=raw[c, g][:], in_=rows.rearrange("(p j) w -> p j w", j=PACK))
+                queue.dma_start(out=raw[c, g][:], in_=rows.rearrange("(p j) w -> p j w", j=PACK))
 
-        def regroup(copy, c, g):
-            grouped[c, g] = grouped_pool.tile(
-                [P, TILES, P, PACK], BF16, name="grouped", tag="grouped", align_bytes=64
-            )
-            copy(
-                out=grouped[c, g][:].rearrange("p i m j -> p m j i"),
-                in_=raw[c, g][:].rearrange("p j (m i) -> p m j i", i=TILES),
+        def regroup(c, g):
+            grouped[c, g] = grouped_pool.tile([P, CHUNK, PACK], BF16, name="grouped", tag="grouped", align_bytes=64)
+            nc.vector.tensor_copy(
+                out=grouped[c, g][:].rearrange("p (w i) j -> p w j i", i=4),
+                in_=raw[c, g][:].rearrange("p j (w i) -> p w j i", i=4),
             )
 
         def quantise(c, g):
@@ -74,7 +73,7 @@ def tile_gat_pa_t_kernel(
             nc.vector.quantize_mx(
                 out=x_codes[c][:, g, :].bitcast(FP8X4),
                 scales=x_scales[c][:, g, :],
-                in_=grouped[c, g][:].rearrange("p i m j -> p (i m j)"),
+                in_=grouped[c, g][:].rearrange("p w j -> p (w j)"),
             )
 
         def project(c, pair):
@@ -99,13 +98,13 @@ def tile_gat_pa_t_kernel(
 
         def add_bias(c, pair):
             if pair == 0:
-                h[c] = h_pool.tile([P, HEADS, TILES, D], F32, name="h", tag="h")
+                h[c] = h_pool.tile([P, TILES, HEADS, D], F32, name="h", tag="h")
             for e in range(PAIR):
                 nc.vector.tensor_tensor(
-                    out=h[c][:, 0:2, pair * PAIR + e, :], in0=acc12[c, pair, e][:], in1=bias[:, 0:2, :], op=ALU.add
+                    out=h[c][:, pair * PAIR + e, 0:2, :], in0=acc12[c, pair, e][:], in1=bias[:, 0:2, :], op=ALU.add
                 )
             nc.vector.tensor_tensor(
-                out=h[c][:, 2, pair * PAIR : (pair + 1) * PAIR, :],
+                out=h[c][:, pair * PAIR : (pair + 1) * PAIR, 2, :],
                 in0=acc3[c, pair][:],
                 in1=bias[:, 2:3, :].to_broadcast([P, PAIR, D]),
                 op=ALU.add,
@@ -116,7 +115,7 @@ def tile_gat_pa_t_kernel(
             for u, (k, e) in enumerate(units):
                 nc.scalar.activation(
                     out=discard[:],
-                    in_=h[c][:, k, pair * PAIR + e, :],
+                    in_=h[c][:, pair * PAIR + e, k, :],
                     func=ACT.Square,
                     accum_out=sums[c, pair][:, u : u + 1],
                 )
@@ -129,23 +128,25 @@ def tile_gat_pa_t_kernel(
             nc.vector.reciprocal(out=inverse[:], in_=floored[:])
             nc.scalar.sqrt(out=rinv[c, pair][:], in_=inverse[:])
 
+        def vector_units(c):
+            return VECTOR_UNITS_LAST if c == CHUNKS - 1 else VECTOR_UNITS
+
         def scale_on_scalar(c, pair):
             for u, (k, e) in enumerate(units):
-                if u >= VECTOR_UNITS:
-                    rows = h[c][:, k, pair * PAIR + e, :]
+                if u >= vector_units(c):
+                    rows = h[c][:, pair * PAIR + e, k, :]
                     nc.scalar.activation(out=rows, in_=rows, func=ACT.Copy, scale=rinv[c, pair][:, u : u + 1])
 
         def scale_on_vector(c, pair):
             for u, (k, e) in enumerate(units):
-                if u < VECTOR_UNITS:
-                    rows = h[c][:, k, pair * PAIR + e, :]
+                if u < vector_units(c):
+                    rows = h[c][:, pair * PAIR + e, k, :]
                     nc.vector.tensor_scalar_mul(out=rows, in0=rows, scalar1=rinv[c, pair][:, u : u + 1])
 
-        def store(c):
-            nc.sync.dma_start(
-                out=out[:, c * CHUNK : (c + 1) * CHUNK, :].rearrange("k (p i) d -> p k (i d)", i=TILES),
-                in_=h[c][:].rearrange("p k i d -> p k (i d)"),
-            )
+        def store(c, pair):
+            for i in range(pair * PAIR, (pair + 1) * PAIR):
+                first = c * CHUNK + i * P
+                nc.sync.dma_start(out=out[:, first : first + P, :].rearrange("k p d -> p k d"), in_=h[c][:, i, :, :])
 
         w_codes = const.tile([P, PASSES, HEADS * D], U32, name="w_codes", align_bytes=64)
         w_scales = const.tile([P, PASSES, HEADS * D], U8, name="w_scales", align_bytes=64)
@@ -161,28 +162,27 @@ def tile_gat_pa_t_kernel(
         nc.vector.memset(warm[:], 1.0)
         nc.scalar.sqrt(out=warm[:], in_=warm[:])
 
-        load(0)
-        for k, (words, scales) in enumerate(((W1_words, W1_scales), (W2_words, W2_scales), (W3_words, W3_scales))):
-            columns = slice(k * D, (k + 1) * D)
-            for quadrant in range(4):
-                nc.sync.dma_start(
-                    out=w_scales[32 * quadrant : 32 * quadrant + 4, :, columns].bitcast(I32),
-                    in_=scales[:, 4 * quadrant : 4 * quadrant + 4, :].rearrange("g q n -> q g n").bitcast(I32),
-                )
-            nc.sync.dma_start(
-                out=w_codes[:, :, columns].bitcast(I32),
-                in_=words.rearrange("g p n t -> p g (n t)").bitcast(I32),
-            )
+        weights = ((W1_words, W1_scales), (W2_words, W2_scales), (W3_words, W3_scales))
         for k, b in enumerate((b1, b2, b3)):
-            nc.scalar.dma_start(out=bias_rows[0:1, k, :], in_=b.rearrange("(o d) -> o d", o=1))
-        for c in range(1, CHUNKS):
-            load(c)
+            nc.gpsimd.dma_start(out=bias_rows[0:1, k, :], in_=b.rearrange("(o d) -> o d", o=1))
+        scale_loads = [(k, quadrant) for k in range(HEADS) for quadrant in range(4)]
+        for c in range(SCALAR_QUEUE_CHUNKS):
+            load(nc.scalar, c)
+            for k, quadrant in scale_loads[6 * c : 6 * c + 6]:
+                nc.sync.dma_start(
+                    out=w_scales[32 * quadrant : 32 * quadrant + 4, :, k * D : (k + 1) * D].bitcast(I32),
+                    in_=weights[k][1][:, 4 * quadrant : 4 * quadrant + 4, :].rearrange("g q n -> q g n").bitcast(I32),
+                )
+        for k in range(HEADS):
+            nc.sync.dma_start(
+                out=w_codes[:, :, k * D : (k + 1) * D].bitcast(I32),
+                in_=weights[k][0].rearrange("g p n t -> p g (n t)").bitcast(I32),
+            )
+        for c in range(SCALAR_QUEUE_CHUNKS, CHUNKS):
+            load(nc.sync, c)
 
-        def pass1_copy(c):
-            return nc.scalar.copy if c < HEAD_CHUNKS else nc.vector.tensor_copy
-
-        regroup(nc.vector.tensor_copy, 0, 0)
-        regroup(pass1_copy(0), 0, 1)
+        regroup(0, 0)
+        regroup(0, 1)
         quantise(0, 0)
         quantise(0, 1)
 
@@ -201,17 +201,18 @@ def tile_gat_pa_t_kernel(
 
         for c in range(CHUNKS + 1):
             if c + 1 < CHUNKS:
-                regroup(nc.vector.tensor_copy, c + 1, 0)
+                regroup(c + 1, 0)
             if c > 0:
                 inverse_norms(c - 1, 1)
                 scale_on_vector(c - 1, 0)
+                store(c - 1, 0)
                 scale_on_scalar(c - 1, 1)
             if c + 1 < CHUNKS:
-                regroup(pass1_copy(c + 1), c + 1, 1)
+                regroup(c + 1, 1)
                 quantise(c + 1, 0)
             if c > 0:
                 scale_on_vector(c - 1, 1)
-                store(c - 1)
+                store(c - 1, 1)
             if c + 1 < CHUNKS:
                 quantise(c + 1, 1)
             if c < CHUNKS:

@@ -28,6 +28,7 @@ EPS = 1e-12
 VECTOR_UNITS = 1
 VECTOR_UNITS_LAST = 3
 SCALAR_QUEUE_CHUNKS = 3
+REGROUP_LEAD = 3
 
 FLOPS = 2 * PIXELS * FEATURES * HEADS * D
 
@@ -51,7 +52,7 @@ def tile_gat_pa_t_kernel(
         ctx.enter_context(tc.manual_schedule())
 
         raw, grouped, x_codes, x_scales = {}, {}, {}, {}
-        acc12, acc3, h, sums, rinv = {}, {}, {}, {}, {}
+        acc12, acc3, h, sums, inverse, rinv = {}, {}, {}, {}, {}, {}
 
         def load(queue, c):
             for g in range(PASSES):
@@ -120,13 +121,15 @@ def tile_gat_pa_t_kernel(
                     accum_out=sums[c, pair][:, u : u + 1],
                 )
 
-        def inverse_norms(c, pair):
+        def invert_sums(c, pair):
             floored = small.tile([P, len(units)], F32, name="floored", tag="floored")
-            inverse = small.tile([P, len(units)], F32, name="inverse", tag="inverse")
-            rinv[c, pair] = small.tile([P, len(units)], F32, name="rinv", tag="rinv")
+            inverse[c, pair] = small.tile([P, len(units)], F32, name="inverse", tag="inverse")
             nc.vector.tensor_scalar_max(out=floored[:], in0=sums[c, pair][:], scalar1=EPS * EPS)
-            nc.vector.reciprocal(out=inverse[:], in_=floored[:])
-            nc.scalar.sqrt(out=rinv[c, pair][:], in_=inverse[:])
+            nc.vector.reciprocal(out=inverse[c, pair][:], in_=floored[:])
+
+        def take_roots(c, pair):
+            rinv[c, pair] = small.tile([P, len(units)], F32, name="rinv", tag="rinv")
+            nc.scalar.sqrt(out=rinv[c, pair][:], in_=inverse[c, pair][:])
 
         def vector_units(c):
             return VECTOR_UNITS_LAST if c == CHUNKS - 1 else VECTOR_UNITS
@@ -181,10 +184,17 @@ def tile_gat_pa_t_kernel(
         for c in range(SCALAR_QUEUE_CHUNKS, CHUNKS):
             load(nc.sync, c)
 
-        regroup(0, 0)
-        regroup(0, 1)
-        quantise(0, 0)
-        quantise(0, 1)
+        steps = [(c, pair) for c in range(CHUNKS) for pair in range(PAIRS)]
+        items = [(c, g) for c in range(CHUNKS) for g in range(PASSES)]
+        def at(sequence, index):
+            return sequence[index : index + 1] if index >= 0 else []
+
+        for c, g in items[:PASSES]:
+            regroup(c, g)
+        for c, g in items[:PASSES]:
+            quantise(c, g)
+        for c, g in items[PASSES:REGROUP_LEAD]:
+            regroup(c, g)
 
         spread12 = psum12.tile([P, 2, D], F32, name="spread12", tag="acc12")
         spread3 = psum3.tile([P, PAIR, D], F32, name="spread3", tag="acc3")
@@ -199,27 +209,22 @@ def tile_gat_pa_t_kernel(
         nc.scalar.copy(out=bias[:, 0:2, :], in_=spread12[:])
         nc.scalar.copy(out=bias[:, 2, :], in_=spread3[:, 0, :])
 
-        for c in range(CHUNKS + 1):
-            if c + 1 < CHUNKS:
-                regroup(c + 1, 0)
-            if c > 0:
-                inverse_norms(c - 1, 1)
-                scale_on_vector(c - 1, 0)
-                store(c - 1, 0)
-                scale_on_scalar(c - 1, 1)
-            if c + 1 < CHUNKS:
-                regroup(c + 1, 1)
-                quantise(c + 1, 0)
-            if c > 0:
-                scale_on_vector(c - 1, 1)
-                store(c - 1, 1)
-            if c + 1 < CHUNKS:
-                quantise(c + 1, 1)
-            if c < CHUNKS:
-                for pair in range(PAIRS):
-                    project(c, pair)
-                for pair in range(PAIRS):
-                    add_bias(c, pair)
-                    square_sums(c, pair)
-                inverse_norms(c, 0)
-                scale_on_scalar(c, 0)
+        project(*steps[0])
+        for q in range(len(steps) + 2):
+            for c, g in at(items, q + REGROUP_LEAD):
+                regroup(c, g)
+            for c, g in at(items, q + REGROUP_LEAD - 1):
+                quantise(c, g)
+            for c, pair in at(steps, q + 1):
+                project(c, pair)
+            for c, pair in at(steps, q - 2):
+                scale_on_scalar(c, pair)
+            for c, pair in at(steps, q):
+                add_bias(c, pair)
+                square_sums(c, pair)
+            for c, pair in at(steps, q - 1):
+                invert_sums(c, pair)
+                take_roots(c, pair)
+            for c, pair in at(steps, q - 2):
+                scale_on_vector(c, pair)
+                store(c, pair)

@@ -25,7 +25,7 @@ CHUNKS = PIXELS // CHUNK
 PAIR = 2
 PAIRS = TILES // PAIR
 EPS = 1e-12
-VECTOR_UNITS = 1
+VECTOR_UNITS = 3
 VECTOR_UNITS_LAST = 3
 SCALAR_QUEUE_CHUNKS = 3
 REGROUP_LEAD = 3

@@ -47,6 +47,7 @@ def tile_gat_pa_t_kernel(
         mx_pool = ctx.enter_context(tc.tile_pool(name="mx", bufs=3))
         h_pool = ctx.enter_context(tc.tile_pool(name="h", bufs=4))
         small = ctx.enter_context(tc.tile_pool(name="small", bufs=4))
+        squares_pool = ctx.enter_context(tc.tile_pool(name="squares", bufs=2))
         psum12 = ctx.enter_context(tc.psum_pool(name="psum12", bufs=2 * PAIR))
         psum3 = ctx.enter_context(tc.psum_pool(name="psum3", bufs=2))
         ctx.enter_context(tc.manual_schedule())
@@ -113,9 +114,10 @@ def tile_gat_pa_t_kernel(
 
         def square_sums(c, pair):
             sums[c, pair] = small.tile([P, len(units)], F32, name="sums", tag="sums")
+            squares = squares_pool.tile([P, len(units), D], F32, name="squares", tag="squares")
             for u, (k, e) in enumerate(units):
                 nc.scalar.activation(
-                    out=discard[:],
+                    out=squares[:, u, :],
                     in_=h[c][:, pair * PAIR + e, k, :],
                     func=ACT.Square,
                     accum_out=sums[c, pair][:, u : u + 1],
@@ -156,7 +158,6 @@ def tile_gat_pa_t_kernel(
         bias_rows = const.tile([P, HEADS, D], BF16, name="bias_rows")
         ones = const.tile([P, P], BF16, name="ones")
         bias = const.tile([P, HEADS, D], F32, name="bias")
-        discard = const.tile([P, D], F32, name="discard")
         warm = const.tile([P, 1], F32, name="warm")
 
         nc.vector.memset(w_scales[:].bitcast(I32), 0)

@@ -25,7 +25,7 @@ CHUNKS = PIXELS // CHUNK
 PAIR = 2
 PAIRS = TILES // PAIR
 EPS = 1e-12
-VECTOR_UNITS = 3
+VECTOR_UNITS = 2
 VECTOR_UNITS_LAST = 3
 SCALAR_QUEUE_CHUNKS = 3
 REGROUP_LEAD = 3
@@ -53,7 +53,7 @@ def tile_gat_pa_t_kernel(
         ctx.enter_context(tc.manual_schedule())
 
         raw, grouped, x_codes, x_scales = {}, {}, {}, {}
-        acc12, acc3, h, sums, inverse, rinv = {}, {}, {}, {}, {}, {}
+        acc12, acc3, h, sums, floored, inverse, rinv = {}, {}, {}, {}, {}, {}, {}
 
         def load(queue, c):
             for g in range(PASSES):
@@ -123,11 +123,13 @@ def tile_gat_pa_t_kernel(
                     accum_out=sums[c, pair][:, u : u + 1],
                 )
 
+        def floor_sums(c, pair):
+            floored[c, pair] = small.tile([P, len(units)], F32, name="floored", tag="floored")
+            nc.vector.tensor_scalar_max(out=floored[c, pair][:], in0=sums[c, pair][:], scalar1=EPS * EPS)
+
         def invert_sums(c, pair):
-            floored = small.tile([P, len(units)], F32, name="floored", tag="floored")
             inverse[c, pair] = small.tile([P, len(units)], F32, name="inverse", tag="inverse")
-            nc.vector.tensor_scalar_max(out=floored[:], in0=sums[c, pair][:], scalar1=EPS * EPS)
-            nc.vector.reciprocal(out=inverse[c, pair][:], in_=floored[:])
+            nc.vector.reciprocal(out=inverse[c, pair][:], in_=floored[c, pair][:])
 
         def take_roots(c, pair):
             rinv[c, pair] = small.tile([P, len(units)], F32, name="rinv", tag="rinv")
@@ -197,6 +199,8 @@ def tile_gat_pa_t_kernel(
         for c, g in items[PASSES:REGROUP_LEAD]:
             regroup(c, g)
 
+        project(*steps[0])
+
         spread12 = psum12.tile([P, 2, D], F32, name="spread12", tag="acc12")
         spread3 = psum3.tile([P, PAIR, D], F32, name="spread3", tag="acc3")
         nc.tensor.matmul(
@@ -210,7 +214,6 @@ def tile_gat_pa_t_kernel(
         nc.scalar.copy(out=bias[:, 0:2, :], in_=spread12[:])
         nc.scalar.copy(out=bias[:, 2, :], in_=spread3[:, 0, :])
 
-        project(*steps[0])
         for q in range(len(steps) + 2):
             for c, g in at(items, q + REGROUP_LEAD):
                 regroup(c, g)
@@ -218,14 +221,15 @@ def tile_gat_pa_t_kernel(
                 quantise(c, g)
             for c, pair in at(steps, q + 1):
                 project(c, pair)
-            for c, pair in at(steps, q - 2):
-                scale_on_scalar(c, pair)
             for c, pair in at(steps, q):
                 add_bias(c, pair)
                 square_sums(c, pair)
             for c, pair in at(steps, q - 1):
-                invert_sums(c, pair)
-                take_roots(c, pair)
+                floor_sums(c, pair)
             for c, pair in at(steps, q - 2):
+                scale_on_scalar(c, pair)
                 scale_on_vector(c, pair)
                 store(c, pair)
+            for c, pair in at(steps, q - 1):
+                invert_sums(c, pair)
+                take_roots(c, pair)

@@ -25,7 +25,7 @@ CHUNKS = PIXELS // CHUNK
 PAIR = 2
 PAIRS = TILES // PAIR
 EPS = 1e-12
-VECTOR_UNITS = 2
+VECTOR_UNITS = 1
 VECTOR_UNITS_LAST = 3
 SCALAR_QUEUE_CHUNKS = 3
 REGROUP_LEAD = 3
@@ -82,14 +82,15 @@ def tile_gat_pa_t_kernel(
             acc3[c, pair] = psum3.tile([P, PAIR, D], F32, name="acc3", tag="acc3")
             for e in range(PAIR):
                 acc12[c, pair, e] = psum12.tile([P, 2, D], F32, name="acc12", tag="acc12")
-                first = (pair * PAIR + e) * P
-                for g in range(PASSES):
-                    for columns, acc in (
-                        (slice(0, 2 * D), acc12[c, pair, e][:].rearrange("p k d -> p (k d)")),
-                        (slice(2 * D, 3 * D), acc3[c, pair][:, e, :]),
-                    ):
+            for columns, banks in (
+                (slice(0, 2 * D), [acc12[c, pair, e][:].rearrange("p k d -> p (k d)") for e in range(PAIR)]),
+                (slice(2 * D, 3 * D), [acc3[c, pair][:, e, :] for e in range(PAIR)]),
+            ):
+                for e in range(PAIR):
+                    first = (pair * PAIR + e) * P
+                    for g in range(PASSES):
                         nc.tensor.matmul_mx(
-                            out=acc,
+                            out=banks[e],
                             lhsT=x_codes[c][:, g, first : first + P].bitcast(FP8X4),
                             lhsT_scale=x_scales[c][:, g, first : first + P],
                             rhs=w_codes[:, g, columns].bitcast(FP8X4),
@@ -171,19 +172,21 @@ def tile_gat_pa_t_kernel(
         weights = ((W1_words, W1_scales), (W2_words, W2_scales), (W3_words, W3_scales))
         for k, b in enumerate((b1, b2, b3)):
             nc.gpsimd.dma_start(out=bias_rows[0:1, k, :], in_=b.rearrange("(o d) -> o d", o=1))
-        scale_loads = [(k, quadrant) for k in range(HEADS) for quadrant in range(4)]
+        weight_loads = [(k, part) for k in range(HEADS) for part in (0, 1, 2, 3, "words")]
         for c in range(SCALAR_QUEUE_CHUNKS):
             load(nc.scalar, c)
-            for k, quadrant in scale_loads[6 * c : 6 * c + 6]:
-                nc.sync.dma_start(
-                    out=w_scales[32 * quadrant : 32 * quadrant + 4, :, k * D : (k + 1) * D].bitcast(I32),
-                    in_=weights[k][1][:, 4 * quadrant : 4 * quadrant + 4, :].rearrange("g q n -> q g n").bitcast(I32),
-                )
-        for k in range(HEADS):
-            nc.sync.dma_start(
-                out=w_codes[:, :, k * D : (k + 1) * D].bitcast(I32),
-                in_=weights[k][0].rearrange("g p n t -> p g (n t)").bitcast(I32),
-            )
+            for k, part in weight_loads[6 * c : 6 * c + 6]:
+                columns = slice(k * D, (k + 1) * D)
+                if part == "words":
+                    nc.sync.dma_start(
+                        out=w_codes[:, :, columns].bitcast(I32),
+                        in_=weights[k][0].rearrange("g p n t -> p g (n t)").bitcast(I32),
+                    )
+                else:
+                    nc.sync.dma_start(
+                        out=w_scales[32 * part : 32 * part + 4, :, columns].bitcast(I32),
+                        in_=weights[k][1][:, 4 * part : 4 * part + 4, :].rearrange("g q n -> q g n").bitcast(I32),
+                    )
         for c in range(SCALAR_QUEUE_CHUNKS, CHUNKS):
             load(nc.sync, c)
 
@@ -199,8 +202,6 @@ def tile_gat_pa_t_kernel(
         for c, g in items[PASSES:REGROUP_LEAD]:
             regroup(c, g)
 
-        project(*steps[0])
-
         spread12 = psum12.tile([P, 2, D], F32, name="spread12", tag="acc12")
         spread3 = psum3.tile([P, PAIR, D], F32, name="spread3", tag="acc3")
         nc.tensor.matmul(
@@ -214,6 +215,7 @@ def tile_gat_pa_t_kernel(
         nc.scalar.copy(out=bias[:, 0:2, :], in_=spread12[:])
         nc.scalar.copy(out=bias[:, 2, :], in_=spread3[:, 0, :])
 
+        project(*steps[0])
         for q in range(len(steps) + 2):
             for c, g in at(items, q + REGROUP_LEAD):
                 regroup(c, g)

@@ -25,10 +25,12 @@ CHUNKS = PIXELS // CHUNK
 PAIR = 2
 PAIRS = TILES // PAIR
 EPS = 1e-12
-VECTOR_UNITS = 1
-VECTOR_UNITS_LAST = 3
+SPLIT_MAIN = (4, 2, 0)
+SPLIT_LATE = (4, 0, 2)
+SPLIT_LAST = (0, 2, 4)
+VECTOR_PIXELS = 304
 SCALAR_QUEUE_CHUNKS = 3
-REGROUP_LEAD = 3
+REGROUP_LEAD = 4
 
 FLOPS = 2 * PIXELS * FEATURES * HEADS * D
 
@@ -53,7 +55,7 @@ def tile_gat_pa_t_kernel(
         ctx.enter_context(tc.manual_schedule())
 
         raw, grouped, x_codes, x_scales = {}, {}, {}, {}
-        acc12, acc3, h, sums, floored, inverse, rinv = {}, {}, {}, {}, {}, {}, {}
+        acc12, acc3, h, sums, inverse, rinv = {}, {}, {}, {}, {}, {}
 
         def load(queue, c):
             for g in range(PASSES):
@@ -64,8 +66,12 @@ def tile_gat_pa_t_kernel(
         def regroup(c, g):
             grouped[c, g] = grouped_pool.tile([P, CHUNK, PACK], BF16, name="grouped", tag="grouped", align_bytes=64)
             nc.vector.tensor_copy(
-                out=grouped[c, g][:].rearrange("p (w i) j -> p w j i", i=4),
-                in_=raw[c, g][:].rearrange("p j (w i) -> p w j i", i=4),
+                out=grouped[c, g][:, :VECTOR_PIXELS, :].rearrange("p (w i) j -> p w j i", i=4),
+                in_=raw[c, g][:, :, :VECTOR_PIXELS].rearrange("p j (w i) -> p w j i", i=4),
+            )
+            nc.scalar.copy(
+                out=grouped[c, g][:, VECTOR_PIXELS:, :].rearrange("p (w i) j -> p w j i", i=4),
+                in_=raw[c, g][:, :, VECTOR_PIXELS:].rearrange("p j (w i) -> p w j i", i=4),
             )
 
         def quantise(c, g):
@@ -124,32 +130,27 @@ def tile_gat_pa_t_kernel(
                     accum_out=sums[c, pair][:, u : u + 1],
                 )
 
-        def floor_sums(c, pair):
-            floored[c, pair] = small.tile([P, len(units)], F32, name="floored", tag="floored")
-            nc.vector.tensor_scalar_max(out=floored[c, pair][:], in0=sums[c, pair][:], scalar1=EPS * EPS)
-
-        def invert_sums(c, pair):
+        def inverse_roots(c, pair):
             inverse[c, pair] = small.tile([P, len(units)], F32, name="inverse", tag="inverse")
-            nc.vector.reciprocal(out=inverse[c, pair][:], in_=floored[c, pair][:])
+            nc.scalar.activation(out=inverse[c, pair][:], in_=sums[c, pair][:], func=ACT.Abs_reciprocal_sqrt)
 
-        def take_roots(c, pair):
+        def cap_inverse(c, pair):
             rinv[c, pair] = small.tile([P, len(units)], F32, name="rinv", tag="rinv")
-            nc.scalar.sqrt(out=rinv[c, pair][:], in_=inverse[c, pair][:])
+            nc.vector.tensor_scalar_min(out=rinv[c, pair][:], in0=inverse[c, pair][:], scalar1=1.0 / EPS)
 
-        def vector_units(c):
-            return VECTOR_UNITS_LAST if c == CHUNKS - 1 else VECTOR_UNITS
-
-        def scale_on_scalar(c, pair):
+        def scale(c, pair, split):
+            on_gpsimd, on_scalar, on_vector = split
             for u, (k, e) in enumerate(units):
-                if u >= vector_units(c):
-                    rows = h[c][:, pair * PAIR + e, k, :]
-                    nc.scalar.activation(out=rows, in_=rows, func=ACT.Copy, scale=rinv[c, pair][:, u : u + 1])
-
-        def scale_on_vector(c, pair):
-            for u, (k, e) in enumerate(units):
-                if u < vector_units(c):
-                    rows = h[c][:, pair * PAIR + e, k, :]
-                    nc.vector.tensor_scalar_mul(out=rows, in0=rows, scalar1=rinv[c, pair][:, u : u + 1])
+                rows = h[c][:, pair * PAIR + e, k, :]
+                factor = rinv[c, pair][:, u : u + 1]
+                if u < on_gpsimd:
+                    nc.gpsimd.tensor_scalar(
+                        out=rows, in0=rows, scalar1=factor, scalar2=0.0, op0=ALU.mult, op1=ALU.add
+                    )
+                elif u < on_gpsimd + on_scalar:
+                    nc.scalar.activation(out=rows, in_=rows, func=ACT.Copy, scale=factor)
+                else:
+                    nc.vector.tensor_scalar_mul(out=rows, in0=rows, scalar1=factor)
 
         def store(c, pair):
             for i in range(pair * PAIR, (pair + 1) * PAIR):
@@ -167,7 +168,7 @@ def tile_gat_pa_t_kernel(
         nc.vector.memset(bias_rows[:], 0.0)
         nc.vector.memset(ones[:], 1.0)
         nc.vector.memset(warm[:], 1.0)
-        nc.scalar.sqrt(out=warm[:], in_=warm[:])
+        nc.scalar.activation(out=warm[:], in_=warm[:], func=ACT.Abs_reciprocal_sqrt)
 
         weights = ((W1_words, W1_scales), (W2_words, W2_scales), (W3_words, W3_scales))
         for k, b in enumerate((b1, b2, b3)):
@@ -195,12 +196,10 @@ def tile_gat_pa_t_kernel(
         def at(sequence, index):
             return sequence[index : index + 1] if index >= 0 else []
 
-        for c, g in items[:PASSES]:
+        for c, g in items[:REGROUP_LEAD]:
             regroup(c, g)
-        for c, g in items[:PASSES]:
-            quantise(c, g)
-        for c, g in items[PASSES:REGROUP_LEAD]:
-            regroup(c, g)
+            for earlier in at(items, items.index((c, g)) - 1):
+                quantise(*earlier)
 
         spread12 = psum12.tile([P, 2, D], F32, name="spread12", tag="acc12")
         spread3 = psum3.tile([P, PAIR, D], F32, name="spread3", tag="acc3")
@@ -215,8 +214,20 @@ def tile_gat_pa_t_kernel(
         nc.scalar.copy(out=bias[:, 0:2, :], in_=spread12[:])
         nc.scalar.copy(out=bias[:, 2, :], in_=spread3[:, 0, :])
 
+        def split_of(q):
+            if q >= len(steps) - 2:
+                return SPLIT_LAST
+            return SPLIT_MAIN if q + 2 + REGROUP_LEAD < len(items) else SPLIT_LATE
+
         project(*steps[0])
         for q in range(len(steps) + 2):
+            for c, pair in at(steps, q):
+                add_bias(c, pair)
+            for c, pair in at(steps, q - 2):
+                scale(c, pair, split_of(q - 2))
+                store(c, pair)
+            for c, pair in at(steps, q):
+                square_sums(c, pair)
             for c, g in at(items, q + REGROUP_LEAD):
                 regroup(c, g)
             for c, g in at(items, q + REGROUP_LEAD - 1):
@@ -224,14 +235,6 @@ def tile_gat_pa_t_kernel(
             for c, pair in at(steps, q + 1):
                 project(c, pair)
             for c, pair in at(steps, q):
-                add_bias(c, pair)
-                square_sums(c, pair)
+                inverse_roots(c, pair)
             for c, pair in at(steps, q - 1):
-                floor_sums(c, pair)
-            for c, pair in at(steps, q - 2):
-                scale_on_scalar(c, pair)
-                scale_on_vector(c, pair)
-                store(c, pair)
-            for c, pair in at(steps, q - 1):
-                invert_sums(c, pair)
-                take_roots(c, pair)
+                cap_inverse(c, pair)

@@ -29,7 +29,6 @@ SPLIT_MAIN = (4, 2, 0)
 SPLIT_LATE = (4, 0, 2)
 SPLIT_LAST = (0, 2, 4)
 VECTOR_PIXELS = 304
-SCALAR_QUEUE_CHUNKS = 3
 REGROUP_LEAD = 4
 
 FLOPS = 2 * PIXELS * FEATURES * HEADS * D
@@ -57,11 +56,10 @@ def tile_gat_pa_t_kernel(
         raw, grouped, x_codes, x_scales = {}, {}, {}, {}
         acc12, acc3, h, sums, inverse, rinv = {}, {}, {}, {}, {}, {}
 
-        def load(queue, c):
-            for g in range(PASSES):
-                raw[c, g] = raw_pool.tile([P, PACK, CHUNK], BF16, name="raw", tag="raw")
-                rows = xf[g * K_PASS : (g + 1) * K_PASS, c * CHUNK : (c + 1) * CHUNK]
-                queue.dma_start(out=raw[c, g][:], in_=rows.rearrange("(p j) w -> p j w", j=PACK))
+        def load(queue, c, g):
+            raw[c, g] = raw_pool.tile([P, PACK, CHUNK], BF16, name="raw", tag="raw")
+            rows = xf[g * K_PASS : (g + 1) * K_PASS, c * CHUNK : (c + 1) * CHUNK]
+            queue.dma_start(out=raw[c, g][:], in_=rows.rearrange("(p j) w -> p j w", j=PACK))
 
         def regroup(c, g):
             grouped[c, g] = grouped_pool.tile([P, CHUNK, PACK], BF16, name="grouped", tag="grouped", align_bytes=64)
@@ -84,26 +82,28 @@ def tile_gat_pa_t_kernel(
                 in_=grouped[c, g][:].rearrange("p w j -> p (w j)"),
             )
 
-        def project(c, pair):
-            acc3[c, pair] = psum3.tile([P, PAIR, D], F32, name="acc3", tag="acc3")
+        def multiply(c, pair, columns, banks):
+            for e in range(PAIR):
+                first = (pair * PAIR + e) * P
+                for g in range(PASSES):
+                    nc.tensor.matmul_mx(
+                        out=banks[e],
+                        lhsT=x_codes[c][:, g, first : first + P].bitcast(FP8X4),
+                        lhsT_scale=x_scales[c][:, g, first : first + P],
+                        rhs=w_codes[:, g, columns].bitcast(FP8X4),
+                        rhs_scale=w_scales[:, g, columns],
+                        start=(g == 0),
+                        stop=(g == PASSES - 1),
+                    )
+
+        def project12(c, pair):
             for e in range(PAIR):
                 acc12[c, pair, e] = psum12.tile([P, 2, D], F32, name="acc12", tag="acc12")
-            for columns, banks in (
-                (slice(0, 2 * D), [acc12[c, pair, e][:].rearrange("p k d -> p (k d)") for e in range(PAIR)]),
-                (slice(2 * D, 3 * D), [acc3[c, pair][:, e, :] for e in range(PAIR)]),
-            ):
-                for e in range(PAIR):
-                    first = (pair * PAIR + e) * P
-                    for g in range(PASSES):
-                        nc.tensor.matmul_mx(
-                            out=banks[e],
-                            lhsT=x_codes[c][:, g, first : first + P].bitcast(FP8X4),
-                            lhsT_scale=x_scales[c][:, g, first : first + P],
-                            rhs=w_codes[:, g, columns].bitcast(FP8X4),
-                            rhs_scale=w_scales[:, g, columns],
-                            start=(g == 0),
-                            stop=(g == PASSES - 1),
-                        )
+            multiply(c, pair, slice(0, 2 * D), [acc12[c, pair, e][:].rearrange("p k d -> p (k d)") for e in range(PAIR)])
+
+        def project3(c, pair):
+            acc3[c, pair] = psum3.tile([P, PAIR, D], F32, name="acc3", tag="acc3")
+            multiply(c, pair, slice(2 * D, 3 * D), [acc3[c, pair][:, e, :] for e in range(PAIR)])
 
         def add_bias(c, pair):
             if pair == 0:
@@ -159,47 +159,56 @@ def tile_gat_pa_t_kernel(
 
         w_codes = const.tile([P, PASSES, HEADS * D], U32, name="w_codes", align_bytes=64)
         w_scales = const.tile([P, PASSES, HEADS * D], U8, name="w_scales", align_bytes=64)
+        staged = const.tile([P, PASSES, HEADS * D], U8, name="staged", align_bytes=64)
         bias_rows = const.tile([P, HEADS, D], BF16, name="bias_rows")
         ones = const.tile([P, P], BF16, name="ones")
         bias = const.tile([P, HEADS, D], F32, name="bias")
         warm = const.tile([P, 1], F32, name="warm")
 
-        nc.vector.memset(w_scales[:].bitcast(I32), 0)
-        nc.vector.memset(bias_rows[:], 0.0)
-        nc.vector.memset(ones[:], 1.0)
-        nc.vector.memset(warm[:], 1.0)
-        nc.scalar.activation(out=warm[:], in_=warm[:], func=ACT.Abs_reciprocal_sqrt)
-
-        weights = ((W1_words, W1_scales), (W2_words, W2_scales), (W3_words, W3_scales))
-        for k, b in enumerate((b1, b2, b3)):
-            nc.gpsimd.dma_start(out=bias_rows[0:1, k, :], in_=b.rearrange("(o d) -> o d", o=1))
-        weight_loads = [(k, part) for k in range(HEADS) for part in (0, 1, 2, 3, "words")]
-        for c in range(SCALAR_QUEUE_CHUNKS):
-            load(nc.scalar, c)
-            for k, part in weight_loads[6 * c : 6 * c + 6]:
-                columns = slice(k * D, (k + 1) * D)
-                if part == "words":
-                    nc.sync.dma_start(
-                        out=w_codes[:, :, columns].bitcast(I32),
-                        in_=weights[k][0].rearrange("g p n t -> p g (n t)").bitcast(I32),
-                    )
-                else:
-                    nc.sync.dma_start(
-                        out=w_scales[32 * part : 32 * part + 4, :, columns].bitcast(I32),
-                        in_=weights[k][1][:, 4 * part : 4 * part + 4, :].rearrange("g q n -> q g n").bitcast(I32),
-                    )
-        for c in range(SCALAR_QUEUE_CHUNKS, CHUNKS):
-            load(nc.sync, c)
-
         steps = [(c, pair) for c in range(CHUNKS) for pair in range(PAIRS)]
         items = [(c, g) for c in range(CHUNKS) for g in range(PASSES)]
+
         def at(sequence, index):
             return sequence[index : index + 1] if index >= 0 else []
 
-        for c, g in items[:REGROUP_LEAD]:
-            regroup(c, g)
-            for earlier in at(items, items.index((c, g)) - 1):
-                quantise(*earlier)
+        words = (W1_words, W2_words, W3_words)
+        scale_bytes = (W1_scales, W2_scales, W3_scales)
+        biases = (b1, b2, b3)
+
+        load(nc.scalar, *items[0])
+        load(nc.scalar, *items[1])
+        nc.vector.memset(bias_rows[:], 0.0)
+        nc.vector.memset(ones[:], 1.0)
+        nc.vector.memset(warm[:], 1.0)
+        nc.vector.memset(w_scales[:].bitcast(I32), 0)
+        nc.scalar.activation(out=warm[:], in_=warm[:], func=ACT.Abs_reciprocal_sqrt)
+        for k in range(HEADS):
+            nc.gpsimd.dma_start(out=bias_rows[0:1, k, :], in_=biases[k].rearrange("(o d) -> o d", o=1))
+        for k in range(HEADS):
+            nc.sync.dma_start(
+                out=staged[0:16, :, k * D : (k + 1) * D].bitcast(I32),
+                in_=scale_bytes[k].rearrange("g q n -> q g n").bitcast(I32),
+            )
+        for k in range(HEADS):
+            nc.sync.dma_start(
+                out=w_codes[:, :, k * D : (k + 1) * D].bitcast(I32),
+                in_=words[k].rearrange("g p n t -> p g (n t)").bitcast(I32),
+            )
+        load(nc.scalar, *items[2])
+        regroup(*items[0])
+        load(nc.scalar, *items[3])
+        regroup(*items[1])
+        quantise(*items[0])
+        for quadrant in range(4):
+            nc.sync.dma_start(
+                out=w_scales[32 * quadrant : 32 * quadrant + 4, :, :].rearrange("p g n -> p (g n)").bitcast(I32),
+                in_=staged[4 * quadrant : 4 * quadrant + 4, :, :].rearrange("p g n -> p (g n)").bitcast(I32),
+            )
+        for c, g in items[4:]:
+            load(nc.sync, c, g)
+        for i in range(2, REGROUP_LEAD):
+            regroup(*items[i])
+            quantise(*items[i - 1])
 
         spread12 = psum12.tile([P, 2, D], F32, name="spread12", tag="acc12")
         spread3 = psum3.tile([P, PAIR, D], F32, name="spread3", tag="acc3")
@@ -210,16 +219,17 @@ def tile_gat_pa_t_kernel(
             start=True,
             stop=True,
         )
-        nc.tensor.matmul(out=spread3[:, 0, :], lhsT=ones[:], rhs=bias_rows[:, 2, :], start=True, stop=True)
         nc.scalar.copy(out=bias[:, 0:2, :], in_=spread12[:])
+        project12(*steps[0])
+        nc.tensor.matmul(out=spread3[:, 0, :], lhsT=ones[:], rhs=bias_rows[:, 2, :], start=True, stop=True)
         nc.scalar.copy(out=bias[:, 2, :], in_=spread3[:, 0, :])
+        project3(*steps[0])
 
         def split_of(q):
             if q >= len(steps) - 2:
                 return SPLIT_LAST
             return SPLIT_MAIN if q + 2 + REGROUP_LEAD < len(items) else SPLIT_LATE
 
-        project(*steps[0])
         for q in range(len(steps) + 2):
             for c, pair in at(steps, q):
                 add_bias(c, pair)
@@ -233,7 +243,8 @@ def tile_gat_pa_t_kernel(
             for c, g in at(items, q + REGROUP_LEAD - 1):
                 quantise(c, g)
             for c, pair in at(steps, q + 1):
-                project(c, pair)
+                project12(c, pair)
+                project3(c, pair)
             for c, pair in at(steps, q):
                 inverse_roots(c, pair)
             for c, pair in at(steps, q - 1):

@@ -25,10 +25,11 @@ CHUNKS = PIXELS // CHUNK
 PAIR = 2
 PAIRS = TILES // PAIR
 EPS = 1e-12
-SPLIT_MAIN = (4, 2, 0)
-SPLIT_LATE = (4, 0, 2)
+SPLIT_MAIN = (0, 4, 2)
+SPLIT_LATE = (3, 1, 2)
 SPLIT_LAST = (0, 2, 4)
-VECTOR_PIXELS = 304
+VECTOR_PIXELS_HEAD = 264
+VECTOR_PIXELS_MAIN = 272
 REGROUP_LEAD = 4
 
 FLOPS = 2 * PIXELS * FEATURES * HEADS * D
@@ -44,7 +45,7 @@ def tile_gat_pa_t_kernel(
     with ExitStack() as ctx:
         const = ctx.enter_context(tc.tile_pool(name="const", bufs=1))
         raw_pool = ctx.enter_context(tc.tile_pool(name="raw", bufs=CHUNKS * PASSES))
-        grouped_pool = ctx.enter_context(tc.tile_pool(name="grouped", bufs=4))
+        grouped_pool = ctx.enter_context(tc.tile_pool(name="grouped", bufs=2))
         mx_pool = ctx.enter_context(tc.tile_pool(name="mx", bufs=3))
         h_pool = ctx.enter_context(tc.tile_pool(name="h", bufs=4))
         small = ctx.enter_context(tc.tile_pool(name="small", bufs=4))
@@ -56,6 +57,17 @@ def tile_gat_pa_t_kernel(
         raw, grouped, x_codes, x_scales = {}, {}, {}, {}
         acc12, acc3, h, sums, inverse, rinv = {}, {}, {}, {}, {}, {}
 
+        steps = [(c, pair) for c in range(CHUNKS) for pair in range(PAIRS)]
+        items = [(c, g) for c in range(CHUNKS) for g in range(PASSES)]
+
+        def at(sequence, index):
+            return sequence[index : index + 1] if index >= 0 else []
+
+        def split_of(q):
+            if q >= len(steps) - 2:
+                return SPLIT_LAST
+            return SPLIT_MAIN if q + 2 + REGROUP_LEAD < len(items) else SPLIT_LATE
+
         def load(queue, c, g):
             raw[c, g] = raw_pool.tile([P, PACK, CHUNK], BF16, name="raw", tag="raw")
             rows = xf[g * K_PASS : (g + 1) * K_PASS, c * CHUNK : (c + 1) * CHUNK]
@@ -63,14 +75,26 @@ def tile_gat_pa_t_kernel(
 
         def regroup(c, g):
             grouped[c, g] = grouped_pool.tile([P, CHUNK, PACK], BF16, name="grouped", tag="grouped", align_bytes=64)
+            in_head = items.index((c, g)) < REGROUP_LEAD
+            cut = VECTOR_PIXELS_HEAD if in_head else VECTOR_PIXELS_MAIN
             nc.vector.tensor_copy(
-                out=grouped[c, g][:, :VECTOR_PIXELS, :].rearrange("p (w i) j -> p w j i", i=4),
-                in_=raw[c, g][:, :, :VECTOR_PIXELS].rearrange("p j (w i) -> p w j i", i=4),
+                out=grouped[c, g][:, :cut, :].rearrange("p (w i) j -> p w j i", i=4),
+                in_=raw[c, g][:, :, :cut].rearrange("p j (w i) -> p w j i", i=4),
             )
-            nc.scalar.copy(
-                out=grouped[c, g][:, VECTOR_PIXELS:, :].rearrange("p (w i) j -> p w j i", i=4),
-                in_=raw[c, g][:, :, VECTOR_PIXELS:].rearrange("p j (w i) -> p w j i", i=4),
-            )
+            if in_head:
+                nc.scalar.copy(
+                    out=grouped[c, g][:, cut:, :].rearrange("p (w i) j -> p w j i", i=4),
+                    in_=raw[c, g][:, :, cut:].rearrange("p j (w i) -> p w j i", i=4),
+                )
+            else:
+                nc.gpsimd.tensor_scalar(
+                    out=grouped[c, g][:, cut:, :],
+                    in0=raw[c, g][:, :, cut:].rearrange("p j w -> p w j"),
+                    scalar1=1.0,
+                    scalar2=0.0,
+                    op0=ALU.mult,
+                    op1=ALU.add,
+                )
 
         def quantise(c, g):
             if g == 0:
@@ -138,12 +162,14 @@ def tile_gat_pa_t_kernel(
             rinv[c, pair] = small.tile([P, len(units)], F32, name="rinv", tag="rinv")
             nc.vector.tensor_scalar_min(out=rinv[c, pair][:], in0=inverse[c, pair][:], scalar1=1.0 / EPS)
 
-        def scale(c, pair, split):
+        def scale(c, pair, split, chosen):
             on_gpsimd, on_scalar, on_vector = split
             for u, (k, e) in enumerate(units):
                 rows = h[c][:, pair * PAIR + e, k, :]
                 factor = rinv[c, pair][:, u : u + 1]
-                if u < on_gpsimd:
+                if u not in chosen:
+                    pass
+                elif u < on_gpsimd:
                     nc.gpsimd.tensor_scalar(
                         out=rows, in0=rows, scalar1=factor, scalar2=0.0, op0=ALU.mult, op1=ALU.add
                     )
@@ -164,12 +190,6 @@ def tile_gat_pa_t_kernel(
         ones = const.tile([P, P], BF16, name="ones")
         bias = const.tile([P, HEADS, D], F32, name="bias")
         warm = const.tile([P, 1], F32, name="warm")
-
-        steps = [(c, pair) for c in range(CHUNKS) for pair in range(PAIRS)]
-        items = [(c, g) for c in range(CHUNKS) for g in range(PASSES)]
-
-        def at(sequence, index):
-            return sequence[index : index + 1] if index >= 0 else []
 
         words = (W1_words, W2_words, W3_words)
         scale_bytes = (W1_scales, W2_scales, W3_scales)
@@ -225,21 +245,24 @@ def tile_gat_pa_t_kernel(
         nc.scalar.copy(out=bias[:, 2, :], in_=spread3[:, 0, :])
         project3(*steps[0])
 
-        def split_of(q):
-            if q >= len(steps) - 2:
-                return SPLIT_LAST
-            return SPLIT_MAIN if q + 2 + REGROUP_LEAD < len(items) else SPLIT_LATE
-
         for q in range(len(steps) + 2):
             for c, pair in at(steps, q):
                 add_bias(c, pair)
             for c, pair in at(steps, q - 2):
-                scale(c, pair, split_of(q - 2))
-                store(c, pair)
+                on_gpsimd, on_scalar, on_vector = split_of(q - 2)
+                late = range(on_gpsimd + on_scalar // 2, on_gpsimd + on_scalar)
+                scale(c, pair, split_of(q - 2), [u for u in range(len(units)) if u not in late])
             for c, pair in at(steps, q):
                 square_sums(c, pair)
+            for c, pair in at(steps, q - 2):
+                scale(c, pair, split_of(q - 2), late)
+                store(c, pair)
             for c, g in at(items, q + REGROUP_LEAD):
                 regroup(c, g)
+            gpsimd_regroups_next = q + 1 + REGROUP_LEAD < len(items)
+            if gpsimd_regroups_next:
+                for c, pair in at(steps, q - 1):
+                    cap_inverse(c, pair)
             for c, g in at(items, q + REGROUP_LEAD - 1):
                 quantise(c, g)
             for c, pair in at(steps, q + 1):
@@ -247,5 +270,6 @@ def tile_gat_pa_t_kernel(
                 project3(c, pair)
             for c, pair in at(steps, q):
                 inverse_roots(c, pair)
-            for c, pair in at(steps, q - 1):
-                cap_inverse(c, pair)
+            if not gpsimd_regroups_next:
+                for c, pair in at(steps, q - 1):
+                    cap_inverse(c, pair)

@@ -26,10 +26,11 @@ PAIR = 2
 PAIRS = TILES // PAIR
 EPS = 1e-12
 SPLIT_MAIN = (0, 4, 2)
-SPLIT_LATE = (3, 1, 2)
+SPLIT_LATE = (3, 0, 3)
 SPLIT_LAST = (0, 2, 4)
-VECTOR_PIXELS_HEAD = 264
-VECTOR_PIXELS_MAIN = 272
+SHARES_HEAD = (240, 272, 0)
+SHARES_EARLY = (184, 88, 240)
+SHARES_MAIN = (248, 24, 240)
 REGROUP_LEAD = 4
 
 FLOPS = 2 * PIXELS * FEATURES * HEADS * D
@@ -75,18 +76,21 @@ def tile_gat_pa_t_kernel(
 
         def regroup(c, g):
             grouped[c, g] = grouped_pool.tile([P, CHUNK, PACK], BF16, name="grouped", tag="grouped", align_bytes=64)
-            in_head = items.index((c, g)) < REGROUP_LEAD
-            cut = VECTOR_PIXELS_HEAD if in_head else VECTOR_PIXELS_MAIN
+            i = items.index((c, g))
+            shares = SHARES_MAIN
+            if i < REGROUP_LEAD + 2:
+                shares = SHARES_HEAD if i < REGROUP_LEAD else SHARES_EARLY
+            on_vector, on_scalar, on_gpsimd = shares
+            cut = on_vector + on_scalar
             nc.vector.tensor_copy(
-                out=grouped[c, g][:, :cut, :].rearrange("p (w i) j -> p w j i", i=4),
-                in_=raw[c, g][:, :, :cut].rearrange("p j (w i) -> p w j i", i=4),
+                out=grouped[c, g][:, :on_vector, :].rearrange("p (w i) j -> p w j i", i=4),
+                in_=raw[c, g][:, :, :on_vector].rearrange("p j (w i) -> p w j i", i=4),
             )
-            if in_head:
-                nc.scalar.copy(
-                    out=grouped[c, g][:, cut:, :].rearrange("p (w i) j -> p w j i", i=4),
-                    in_=raw[c, g][:, :, cut:].rearrange("p j (w i) -> p w j i", i=4),
-                )
-            else:
+            nc.scalar.copy(
+                out=grouped[c, g][:, on_vector:cut, :].rearrange("p (w i) j -> p w j i", i=4),
+                in_=raw[c, g][:, :, on_vector:cut].rearrange("p j (w i) -> p w j i", i=4),
+            )
+            if on_gpsimd > 0:
                 nc.gpsimd.tensor_scalar(
                     out=grouped[c, g][:, cut:, :],
                     in0=raw[c, g][:, :, cut:].rearrange("p j w -> p w j"),

@@ -56,7 +56,7 @@ def tile_gat_pa_t_kernel(
         ctx.enter_context(tc.manual_schedule())
 
         raw, grouped, x_codes, x_scales = {}, {}, {}, {}
-        acc12, acc3, h, sums, inverse, rinv = {}, {}, {}, {}, {}, {}
+        acc12, acc3, h, sums, squares, inverse, rinv = {}, {}, {}, {}, {}, {}, {}
 
         steps = [(c, pair) for c in range(CHUNKS) for pair in range(PAIRS)]
         items = [(c, g) for c in range(CHUNKS) for g in range(PASSES)]
@@ -147,12 +147,14 @@ def tile_gat_pa_t_kernel(
                 op=ALU.add,
             )
 
-        def square_sums(c, pair):
-            sums[c, pair] = small.tile([P, len(units)], F32, name="sums", tag="sums")
-            squares = squares_pool.tile([P, len(units), D], F32, name="squares", tag="squares")
-            for u, (k, e) in enumerate(units):
+        def square_sums(c, pair, chosen):
+            if 0 in chosen:
+                sums[c, pair] = small.tile([P, len(units)], F32, name="sums", tag="sums")
+                squares[c, pair] = squares_pool.tile([P, len(units), D], F32, name="squares", tag="squares")
+            for u in chosen:
+                k, e = units[u]
                 nc.scalar.activation(
-                    out=squares[:, u, :],
+                    out=squares[c, pair][:, u, :],
                     in_=h[c][:, pair * PAIR + e, k, :],
                     func=ACT.Square,
                     accum_out=sums[c, pair][:, u : u + 1],
@@ -181,6 +183,14 @@ def tile_gat_pa_t_kernel(
                     nc.scalar.activation(out=rows, in_=rows, func=ACT.Copy, scale=factor)
                 else:
                     nc.vector.tensor_scalar_mul(out=rows, in0=rows, scalar1=factor)
+
+        def store_by_units(c, pair, split):
+            on_gpsimd, on_scalar, on_vector = split
+            ready = [(3 * (u + 1), u) for u in range(on_scalar)] + [(2 * (v + 1), on_scalar + v) for v in range(on_vector)]
+            for when, u in sorted(ready):
+                k, e = units[u]
+                first = c * CHUNK + (pair * PAIR + e) * P
+                nc.sync.dma_start(out=out[k, first : first + P, :], in_=h[c][:, pair * PAIR + e, k, :])
 
         def store(c, pair):
             for i in range(pair * PAIR, (pair + 1) * PAIR):
@@ -257,10 +267,17 @@ def tile_gat_pa_t_kernel(
                 late = range(on_gpsimd + on_scalar // 2, on_gpsimd + on_scalar)
                 scale(c, pair, split_of(q - 2), [u for u in range(len(units)) if u not in late])
             for c, pair in at(steps, q):
-                square_sums(c, pair)
+                square_sums(c, pair, range(0, 2))
+            for c, pair in at(steps, q - 1):
+                inverse_roots(c, pair)
+            for c, pair in at(steps, q):
+                square_sums(c, pair, range(2, len(units)))
             for c, pair in at(steps, q - 2):
                 scale(c, pair, split_of(q - 2), late)
-                store(c, pair)
+                if (c, pair) == steps[-1]:
+                    store_by_units(c, pair, split_of(q - 2))
+                else:
+                    store(c, pair)
             for c, g in at(items, q + REGROUP_LEAD):
                 regroup(c, g)
             gpsimd_regroups_next = q + 1 + REGROUP_LEAD < len(items)
@@ -272,8 +289,6 @@ def tile_gat_pa_t_kernel(
             for c, pair in at(steps, q + 1):
                 project12(c, pair)
                 project3(c, pair)
-            for c, pair in at(steps, q):
-                inverse_roots(c, pair)
             if not gpsimd_regroups_next:
                 for c, pair in at(steps, q - 1):
                     cap_inverse(c, pair)

@@ -1,6 +1,7 @@
 from contextlib import ExitStack
 
 import concourse.mybir as mybir
+from concourse.masks import make_identity
 
 F32 = mybir.dt.float32
 BF16 = mybir.dt.bfloat16
@@ -25,12 +26,13 @@ CHUNKS = PIXELS // CHUNK
 PAIR = 2
 PAIRS = TILES // PAIR
 EPS = 1e-12
-SPLIT_MAIN = (0, 4, 2)
+SPLIT_MAIN = (0, 2, 4)
 SPLIT_LATE = (3, 0, 3)
 SPLIT_LAST = (0, 2, 4)
-SHARES_HEAD = (240, 272, 0)
-SHARES_EARLY = (184, 88, 240)
-SHARES_MAIN = (248, 24, 240)
+SHARES_HEAD = (160, 96, 0)
+SHARES_EARLY = (0, 0, 256)
+SHARES_MAIN = (0, 0, 256)
+PE_PIXELS = 256
 REGROUP_LEAD = 4
 
 FLOPS = 2 * PIXELS * FEATURES * HEADS * D
@@ -52,10 +54,11 @@ def tile_gat_pa_t_kernel(
         small = ctx.enter_context(tc.tile_pool(name="small", bufs=4))
         squares_pool = ctx.enter_context(tc.tile_pool(name="squares", bufs=2))
         psum12 = ctx.enter_context(tc.psum_pool(name="psum12", bufs=2 * PAIR))
+        psum_x = ctx.enter_context(tc.psum_pool(name="psum_x", bufs=2))
         psum3 = ctx.enter_context(tc.psum_pool(name="psum3", bufs=2))
         ctx.enter_context(tc.manual_schedule())
 
-        raw, grouped, x_codes, x_scales = {}, {}, {}, {}
+        raw, grouped, x_codes, x_scales, mixed = {}, {}, {}, {}, {}
         acc12, acc3, h, sums, squares, inverse, rinv = {}, {}, {}, {}, {}, {}, {}
 
         steps = [(c, pair) for c in range(CHUNKS) for pair in range(PAIRS)]
@@ -74,22 +77,40 @@ def tile_gat_pa_t_kernel(
             rows = xf[g * K_PASS : (g + 1) * K_PASS, c * CHUNK : (c + 1) * CHUNK]
             queue.dma_start(out=raw[c, g][:], in_=rows.rearrange("(p j) w -> p j w", j=PACK))
 
+        def shares_of(c, g):
+            i = items.index((c, g))
+            if i < REGROUP_LEAD:
+                return SHARES_HEAD
+            return SHARES_EARLY if i < REGROUP_LEAD + 2 else SHARES_MAIN
+
+        def interleave(c, g):
+            mixed[c, g] = psum_x.tile([P, PE_PIXELS, PACK], BF16, name="mixed", tag="mixed")
+            first = sum(shares_of(c, g)[:2])
+            for w in range(0, PE_PIXELS, P):
+                nc.tensor.matmul(
+                    out=mixed[c, g][:, w : w + P, :],
+                    lhsT=identity[:],
+                    rhs=raw[c, g][:, :, first + w : first + w + P].rearrange("p j w -> p w j"),
+                    start=True,
+                    stop=True,
+                )
+
         def regroup(c, g):
             grouped[c, g] = grouped_pool.tile([P, CHUNK, PACK], BF16, name="grouped", tag="grouped", align_bytes=64)
-            i = items.index((c, g))
-            shares = SHARES_MAIN
-            if i < REGROUP_LEAD + 2:
-                shares = SHARES_HEAD if i < REGROUP_LEAD else SHARES_EARLY
-            on_vector, on_scalar, on_gpsimd = shares
+            on_vector, on_scalar, on_gpsimd = shares_of(c, g)
             cut = on_vector + on_scalar
-            nc.vector.tensor_copy(
-                out=grouped[c, g][:, :on_vector, :].rearrange("p (w i) j -> p w j i", i=4),
-                in_=raw[c, g][:, :, :on_vector].rearrange("p j (w i) -> p w j i", i=4),
-            )
-            nc.scalar.copy(
-                out=grouped[c, g][:, on_vector:cut, :].rearrange("p (w i) j -> p w j i", i=4),
-                in_=raw[c, g][:, :, on_vector:cut].rearrange("p j (w i) -> p w j i", i=4),
-            )
+            if on_vector > 0:
+                nc.vector.tensor_copy(
+                    out=grouped[c, g][:, :on_vector, :].rearrange("p (w i) j -> p w j i", i=4),
+                    in_=raw[c, g][:, :, :on_vector].rearrange("p j (w i) -> p w j i", i=4),
+                )
+            nc.scalar.copy(out=grouped[c, g][:, cut : cut + PE_PIXELS, :], in_=mixed[c, g][:])
+            if on_scalar > 0:
+                nc.scalar.copy(
+                    out=grouped[c, g][:, on_vector:cut, :].rearrange("p (w i) j -> p w j i", i=4),
+                    in_=raw[c, g][:, :, on_vector:cut].rearrange("p j (w i) -> p w j i", i=4),
+                )
+            cut += PE_PIXELS
             if on_gpsimd > 0:
                 nc.gpsimd.tensor_scalar(
                     out=grouped[c, g][:, cut:, :],
@@ -204,6 +225,7 @@ def tile_gat_pa_t_kernel(
         ones = const.tile([P, P], BF16, name="ones")
         bias = const.tile([P, HEADS, D], F32, name="bias")
         warm = const.tile([P, 1], F32, name="warm")
+        identity = const.tile([P, P], BF16, name="identity")
 
         words = (W1_words, W2_words, W3_words)
         scale_bytes = (W1_scales, W2_scales, W3_scales)
@@ -216,6 +238,7 @@ def tile_gat_pa_t_kernel(
         nc.vector.memset(warm[:], 1.0)
         nc.vector.memset(w_scales[:].bitcast(I32), 0)
         nc.scalar.activation(out=warm[:], in_=warm[:], func=ACT.Abs_reciprocal_sqrt)
+        make_identity(nc, identity[:])
         for k in range(HEADS):
             nc.gpsimd.dma_start(out=bias_rows[0:1, k, :], in_=biases[k].rearrange("(o d) -> o d", o=1))
         for k in range(HEADS):
@@ -229,8 +252,10 @@ def tile_gat_pa_t_kernel(
                 in_=words[k].rearrange("g p n t -> p g (n t)").bitcast(I32),
             )
         load(nc.scalar, *items[2])
+        interleave(*items[0])
         regroup(*items[0])
         load(nc.scalar, *items[3])
+        interleave(*items[1])
         regroup(*items[1])
         quantise(*items[0])
         for quadrant in range(4):
@@ -241,6 +266,7 @@ def tile_gat_pa_t_kernel(
         for c, g in items[4:]:
             load(nc.sync, c, g)
         for i in range(2, REGROUP_LEAD):
+            interleave(*items[i])
             regroup(*items[i])
             quantise(*items[i - 1])
 
@@ -258,6 +284,7 @@ def tile_gat_pa_t_kernel(
         nc.tensor.matmul(out=spread3[:, 0, :], lhsT=ones[:], rhs=bias_rows[:, 2, :], start=True, stop=True)
         nc.scalar.copy(out=bias[:, 2, :], in_=spread3[:, 0, :])
         project3(*steps[0])
+        interleave(*items[REGROUP_LEAD])
 
         for q in range(len(steps) + 2):
             for c, pair in at(steps, q):
@@ -289,6 +316,8 @@ def tile_gat_pa_t_kernel(
             for c, pair in at(steps, q + 1):
                 project12(c, pair)
                 project3(c, pair)
+            for c, g in at(items, q + 1 + REGROUP_LEAD):
+                interleave(c, g)
             if not gpsimd_regroups_next:
                 for c, pair in at(steps, q - 1):
                     cap_inverse(c, pair)

@@ -88,9 +88,9 @@ def tile_gat_pa_t_kernel(
             first = sum(shares_of(c, g)[:2])
             for w in range(0, PE_PIXELS, P):
                 nc.tensor.matmul(
-                    out=mixed[c, g][:, w : w + P, :],
+                    out=mixed[c, g][:, w : w + P, :].rearrange("p w (h t) -> p h w t", t=2),
                     lhsT=identity[:],
-                    rhs=raw[c, g][:, :, first + w : first + w + P].rearrange("p j w -> p w j"),
+                    rhs=raw[c, g][:, :, first + w : first + w + P].rearrange("p (h t) w -> p h w t", t=2),
                     start=True,
                     stop=True,
                 )

@@ -29,8 +29,8 @@ EPS = 1e-12
 SPLIT_MAIN = (0, 2, 4)
 SPLIT_LATE = (3, 0, 3)
 SPLIT_LAST = (0, 2, 4)
-SHARES_HEAD = (160, 96, 0)
-SHARES_EARLY = (0, 0, 256)
+SHARES_HEAD = (240, 272, 0)
+SHARES_EARLY = (184, 88, 240)
 SHARES_MAIN = (0, 0, 256)
 PE_PIXELS = 256
 REGROUP_LEAD = 4
@@ -84,6 +84,8 @@ def tile_gat_pa_t_kernel(
             return SHARES_EARLY if i < REGROUP_LEAD + 2 else SHARES_MAIN
 
         def interleave(c, g):
+            if sum(shares_of(c, g)) == CHUNK:
+                return
             mixed[c, g] = psum_x.tile([P, PE_PIXELS, PACK], BF16, name="mixed", tag="mixed")
             first = sum(shares_of(c, g)[:2])
             for w in range(0, PE_PIXELS, P):
@@ -104,13 +106,14 @@ def tile_gat_pa_t_kernel(
                     out=grouped[c, g][:, :on_vector, :].rearrange("p (w i) j -> p w j i", i=4),
                     in_=raw[c, g][:, :, :on_vector].rearrange("p j (w i) -> p w j i", i=4),
                 )
-            nc.scalar.copy(out=grouped[c, g][:, cut : cut + PE_PIXELS, :], in_=mixed[c, g][:])
+            if (c, g) in mixed:
+                nc.scalar.copy(out=grouped[c, g][:, cut : cut + PE_PIXELS, :], in_=mixed[c, g][:])
             if on_scalar > 0:
                 nc.scalar.copy(
                     out=grouped[c, g][:, on_vector:cut, :].rearrange("p (w i) j -> p w j i", i=4),
                     in_=raw[c, g][:, :, on_vector:cut].rearrange("p j (w i) -> p w j i", i=4),
                 )
-            cut += PE_PIXELS
+            cut = CHUNK - on_gpsimd
             if on_gpsimd > 0:
                 nc.gpsimd.tensor_scalar(
                     out=grouped[c, g][:, cut:, :],
@@ -238,9 +241,9 @@ def tile_gat_pa_t_kernel(
         nc.vector.memset(warm[:], 1.0)
         nc.vector.memset(w_scales[:].bitcast(I32), 0)
         nc.scalar.activation(out=warm[:], in_=warm[:], func=ACT.Abs_reciprocal_sqrt)
-        make_identity(nc, identity[:])
         for k in range(HEADS):
             nc.gpsimd.dma_start(out=bias_rows[0:1, k, :], in_=biases[k].rearrange("(o d) -> o d", o=1))
+        make_identity(nc, identity[:])
         for k in range(HEADS):
             nc.sync.dma_start(
                 out=staged[0:16, :, k * D : (k + 1) * D].bitcast(I32),

@@ -29,8 +29,8 @@ EPS = 1e-12
 SPLIT_MAIN = (0, 2, 4)
 SPLIT_LATE = (3, 0, 3)
 SPLIT_LAST = (0, 2, 4)
-SHARES_HEAD = (240, 272, 0)
-SHARES_EARLY = (184, 88, 240)
+SHARES_HEAD = (336, 176, 0)
+SHARES_FIRST = (256, 0, 0)
 SHARES_MAIN = (0, 0, 256)
 PE_PIXELS = 256
 REGROUP_LEAD = 4
@@ -81,7 +81,7 @@ def tile_gat_pa_t_kernel(
             i = items.index((c, g))
             if i < REGROUP_LEAD:
                 return SHARES_HEAD
-            return SHARES_EARLY if i < REGROUP_LEAD + 2 else SHARES_MAIN
+            return SHARES_FIRST if i == REGROUP_LEAD else SHARES_MAIN
 
         def interleave(c, g):
             if sum(shares_of(c, g)) == CHUNK:
@@ -234,58 +234,61 @@ def tile_gat_pa_t_kernel(
         scale_bytes = (W1_scales, W2_scales, W3_scales)
         biases = (b1, b2, b3)
 
-        load(nc.scalar, *items[0])
-        load(nc.scalar, *items[1])
-        nc.vector.memset(bias_rows[:], 0.0)
-        nc.vector.memset(ones[:], 1.0)
-        nc.vector.memset(warm[:], 1.0)
+        def load_words(k):
+            nc.sync.dma_start(
+                out=w_codes[:, :, k * D : (k + 1) * D].bitcast(I32),
+                in_=words[k].rearrange("g p n t -> p g (n t)").bitcast(I32),
+            )
+
+        def spread_biases():
+            spread12 = psum12.tile([P, 2, D], F32, name="spread12", tag="acc12")
+            spread3 = psum3.tile([P, PAIR, D], F32, name="spread3", tag="acc3")
+            nc.tensor.matmul(
+                out=spread12[:].rearrange("p k d -> p (k d)"),
+                lhsT=ones[:],
+                rhs=bias_rows[:, 0:2, :].rearrange("p k d -> p (k d)"),
+                start=True,
+                stop=True,
+            )
+            nc.tensor.matmul(out=spread3[:, 0, :], lhsT=ones[:], rhs=bias_rows[:, 2, :], start=True, stop=True)
+            nc.scalar.copy(out=bias[:, 0:2, :], in_=spread12[:])
+            nc.scalar.copy(out=bias[:, 2, :], in_=spread3[:, 0, :])
+
         nc.vector.memset(w_scales[:].bitcast(I32), 0)
-        nc.scalar.activation(out=warm[:], in_=warm[:], func=ACT.Abs_reciprocal_sqrt)
-        for k in range(HEADS):
-            nc.gpsimd.dma_start(out=bias_rows[0:1, k, :], in_=biases[k].rearrange("(o d) -> o d", o=1))
-        make_identity(nc, identity[:])
         for k in range(HEADS):
             nc.sync.dma_start(
                 out=staged[0:16, :, k * D : (k + 1) * D].bitcast(I32),
                 in_=scale_bytes[k].rearrange("g q n -> q g n").bitcast(I32),
             )
-        for k in range(HEADS):
-            nc.sync.dma_start(
-                out=w_codes[:, :, k * D : (k + 1) * D].bitcast(I32),
-                in_=words[k].rearrange("g p n t -> p g (n t)").bitcast(I32),
-            )
+        load(nc.scalar, *items[0])
+        load(nc.scalar, *items[1])
+        load_words(0)
         load(nc.scalar, *items[2])
-        interleave(*items[0])
-        regroup(*items[0])
         load(nc.scalar, *items[3])
-        interleave(*items[1])
-        regroup(*items[1])
-        quantise(*items[0])
+        nc.vector.memset(bias_rows[:], 0.0)
+        nc.vector.memset(ones[:], 1.0)
+        nc.vector.memset(warm[:], 1.0)
+        nc.scalar.activation(out=warm[:], in_=warm[:], func=ACT.Abs_reciprocal_sqrt)
+        for k in range(HEADS):
+            nc.gpsimd.dma_start(out=bias_rows[0:1, k, :], in_=biases[k].rearrange("(o d) -> o d", o=1))
+        make_identity(nc, identity[:])
         for quadrant in range(4):
             nc.sync.dma_start(
                 out=w_scales[32 * quadrant : 32 * quadrant + 4, :, :].rearrange("p g n -> p (g n)").bitcast(I32),
                 in_=staged[4 * quadrant : 4 * quadrant + 4, :, :].rearrange("p g n -> p (g n)").bitcast(I32),
             )
+        load_words(1)
+        load_words(2)
         for c, g in items[4:]:
             load(nc.sync, c, g)
-        for i in range(2, REGROUP_LEAD):
-            interleave(*items[i])
+        regroup(*items[0])
+        for i in range(1, REGROUP_LEAD):
+            if i == REGROUP_LEAD - 1:
+                spread_biases()
             regroup(*items[i])
             quantise(*items[i - 1])
 
-        spread12 = psum12.tile([P, 2, D], F32, name="spread12", tag="acc12")
-        spread3 = psum3.tile([P, PAIR, D], F32, name="spread3", tag="acc3")
-        nc.tensor.matmul(
-            out=spread12[:].rearrange("p k d -> p (k d)"),
-            lhsT=ones[:],
-            rhs=bias_rows[:, 0:2, :].rearrange("p k d -> p (k d)"),
-            start=True,
-            stop=True,
-        )
-        nc.scalar.copy(out=bias[:, 0:2, :], in_=spread12[:])
         project12(*steps[0])
-        nc.tensor.matmul(out=spread3[:, 0, :], lhsT=ones[:], rhs=bias_rows[:, 2, :], start=True, stop=True)
-        nc.scalar.copy(out=bias[:, 2, :], in_=spread3[:, 0, :])
         project3(*steps[0])
         interleave(*items[REGROUP_LEAD])
 

@@ -29,8 +29,9 @@ EPS = 1e-12
 SPLIT_MAIN = (0, 2, 4)
 SPLIT_LATE = (3, 0, 3)
 SPLIT_LAST = (0, 2, 4)
-SHARES_HEAD = (336, 176, 0)
+SHARES_HEAD = (272, 240, 0)
 SHARES_FIRST = (256, 0, 0)
+SHARES_SECOND = (184, 88, 240)
 SHARES_MAIN = (0, 0, 256)
 PE_PIXELS = 256
 REGROUP_LEAD = 4
@@ -81,7 +82,9 @@ def tile_gat_pa_t_kernel(
             i = items.index((c, g))
             if i < REGROUP_LEAD:
                 return SHARES_HEAD
-            return SHARES_FIRST if i == REGROUP_LEAD else SHARES_MAIN
+            if i == REGROUP_LEAD:
+                return SHARES_FIRST
+            return SHARES_SECOND if i == REGROUP_LEAD + 1 else SHARES_MAIN
 
         def interleave(c, g):
             if sum(shares_of(c, g)) == CHUNK:

from contextlib import ExitStack

import concourse.mybir as mybir
from concourse.masks import make_identity

F32 = mybir.dt.float32
BF16 = mybir.dt.bfloat16
I32 = mybir.dt.int32
U32 = mybir.dt.uint32
U8 = mybir.dt.uint8
FP8X4 = mybir.dt.float8_e4m3fn_x4
ACT = mybir.ActivationFunctionType
ALU = mybir.AluOpType

P = 128
PACK = 4
K_PASS = P * PACK
FEATURES = 1024
PASSES = FEATURES // K_PASS
PIXELS = 64 * 64
HEADS = 3
D = 256
TILES = 4
CHUNK = TILES * P
CHUNKS = PIXELS // CHUNK
PAIR = 2
PAIRS = TILES // PAIR
EPS = 1e-12
SPLIT_MAIN = (0, 2, 4)
SPLIT_LATE = (3, 0, 3)
SPLIT_LAST = (0, 2, 4)
SHARES_HEAD = (272, 240, 0)
SHARES_FIRST = (256, 0, 0)
SHARES_SECOND = (184, 88, 240)
SHARES_MAIN = (0, 0, 256)
PE_PIXELS = 256
REGROUP_LEAD = 4

FLOPS = 2 * PIXELS * FEATURES * HEADS * D


def tile_gat_pa_t_kernel(
    tc, x, W1_words, W1_scales, b1, W2_words, W2_scales, b2, W3_words, W3_scales, b3, out
):
    nc = tc.nc
    xf = x.rearrange("b f i j -> (b f) (i j)")
    units = [(k, e) for e in range(PAIR) for k in (0, 1)] + [(2, e) for e in range(PAIR)]

    with ExitStack() as ctx:
        const = ctx.enter_context(tc.tile_pool(name="const", bufs=1))
        raw_pool = ctx.enter_context(tc.tile_pool(name="raw", bufs=CHUNKS * PASSES))
        grouped_pool = ctx.enter_context(tc.tile_pool(name="grouped", bufs=2))
        mx_pool = ctx.enter_context(tc.tile_pool(name="mx", bufs=3))
        h_pool = ctx.enter_context(tc.tile_pool(name="h", bufs=4))
        small = ctx.enter_context(tc.tile_pool(name="small", bufs=4))
        squares_pool = ctx.enter_context(tc.tile_pool(name="squares", bufs=2))
        psum12 = ctx.enter_context(tc.psum_pool(name="psum12", bufs=2 * PAIR))
        psum_x = ctx.enter_context(tc.psum_pool(name="psum_x", bufs=2))
        psum3 = ctx.enter_context(tc.psum_pool(name="psum3", bufs=2))
        ctx.enter_context(tc.manual_schedule())

        raw, grouped, x_codes, x_scales, mixed = {}, {}, {}, {}, {}
        acc12, acc3, h, sums, squares, inverse, rinv = {}, {}, {}, {}, {}, {}, {}

        steps = [(c, pair) for c in range(CHUNKS) for pair in range(PAIRS)]
        items = [(c, g) for c in range(CHUNKS) for g in range(PASSES)]

        def at(sequence, index):
            return sequence[index : index + 1] if index >= 0 else []

        def split_of(q):
            if q >= len(steps) - 2:
                return SPLIT_LAST
            return SPLIT_MAIN if q + 2 + REGROUP_LEAD < len(items) else SPLIT_LATE

        def load(queue, c, g):
            raw[c, g] = raw_pool.tile([P, PACK, CHUNK], BF16, name="raw", tag="raw")
            rows = xf[g * K_PASS : (g + 1) * K_PASS, c * CHUNK : (c + 1) * CHUNK]
            queue.dma_start(out=raw[c, g][:], in_=rows.rearrange("(p j) w -> p j w", j=PACK))

        def shares_of(c, g):
            i = items.index((c, g))
            if i < REGROUP_LEAD:
                return SHARES_HEAD
            if i == REGROUP_LEAD:
                return SHARES_FIRST
            return SHARES_SECOND if i == REGROUP_LEAD + 1 else SHARES_MAIN

        def interleave(c, g):
            if sum(shares_of(c, g)) == CHUNK:
                return
            mixed[c, g] = psum_x.tile([P, PE_PIXELS, PACK], BF16, name="mixed", tag="mixed")
            first = sum(shares_of(c, g)[:2])
            for w in range(0, PE_PIXELS, P):
                nc.tensor.matmul(
                    out=mixed[c, g][:, w : w + P, :].rearrange("p w (h t) -> p h w t", t=2),
                    lhsT=identity[:],
                    rhs=raw[c, g][:, :, first + w : first + w + P].rearrange("p (h t) w -> p h w t", t=2),
                    start=True,
                    stop=True,
                )

        def regroup(c, g):
            grouped[c, g] = grouped_pool.tile([P, CHUNK, PACK], BF16, name="grouped", tag="grouped", align_bytes=64)
            on_vector, on_scalar, on_gpsimd = shares_of(c, g)
            cut = on_vector + on_scalar
            if on_vector > 0:
                nc.vector.tensor_copy(
                    out=grouped[c, g][:, :on_vector, :].rearrange("p (w i) j -> p w j i", i=4),
                    in_=raw[c, g][:, :, :on_vector].rearrange("p j (w i) -> p w j i", i=4),
                )
            if (c, g) in mixed:
                nc.scalar.copy(out=grouped[c, g][:, cut : cut + PE_PIXELS, :], in_=mixed[c, g][:])
            if on_scalar > 0:
                nc.scalar.copy(
                    out=grouped[c, g][:, on_vector:cut, :].rearrange("p (w i) j -> p w j i", i=4),
                    in_=raw[c, g][:, :, on_vector:cut].rearrange("p j (w i) -> p w j i", i=4),
                )
            cut = CHUNK - on_gpsimd
            if on_gpsimd > 0:
                nc.gpsimd.tensor_scalar(
                    out=grouped[c, g][:, cut:, :],
                    in0=raw[c, g][:, :, cut:].rearrange("p j w -> p w j"),
                    scalar1=1.0,
                    scalar2=0.0,
                    op0=ALU.mult,
                    op1=ALU.add,
                )

        def quantise(c, g):
            if g == 0:
                x_codes[c] = mx_pool.tile([P, PASSES, CHUNK], U32, name="x_codes", tag="x_codes", align_bytes=64)
                x_scales[c] = mx_pool.tile([P, PASSES, CHUNK], U8, name="x_scales", tag="x_scales", align_bytes=64)
            nc.vector.quantize_mx(
                out=x_codes[c][:, g, :].bitcast(FP8X4),
                scales=x_scales[c][:, g, :],
                in_=grouped[c, g][:].rearrange("p w j -> p (w j)"),
            )

        def multiply(c, pair, columns, banks):
            for e in range(PAIR):
                first = (pair * PAIR + e) * P
                for g in range(PASSES):
                    nc.tensor.matmul_mx(
                        out=banks[e],
                        lhsT=x_codes[c][:, g, first : first + P].bitcast(FP8X4),
                        lhsT_scale=x_scales[c][:, g, first : first + P],
                        rhs=w_codes[:, g, columns].bitcast(FP8X4),
                        rhs_scale=w_scales[:, g, columns],
                        start=(g == 0),
                        stop=(g == PASSES - 1),
                    )

        def project12(c, pair):
            for e in range(PAIR):
                acc12[c, pair, e] = psum12.tile([P, 2, D], F32, name="acc12", tag="acc12")
            multiply(c, pair, slice(0, 2 * D), [acc12[c, pair, e][:].rearrange("p k d -> p (k d)") for e in range(PAIR)])

        def project3(c, pair):
            acc3[c, pair] = psum3.tile([P, PAIR, D], F32, name="acc3", tag="acc3")
            multiply(c, pair, slice(2 * D, 3 * D), [acc3[c, pair][:, e, :] for e in range(PAIR)])

        def add_bias(c, pair):
            if pair == 0:
                h[c] = h_pool.tile([P, TILES, HEADS, D], F32, name="h", tag="h")
            for e in range(PAIR):
                nc.vector.tensor_tensor(
                    out=h[c][:, pair * PAIR + e, 0:2, :], in0=acc12[c, pair, e][:], in1=bias[:, 0:2, :], op=ALU.add
                )
            nc.vector.tensor_tensor(
                out=h[c][:, pair * PAIR : (pair + 1) * PAIR, 2, :],
                in0=acc3[c, pair][:],
                in1=bias[:, 2:3, :].to_broadcast([P, PAIR, D]),
                op=ALU.add,
            )

        def square_sums(c, pair, chosen):
            if 0 in chosen:
                sums[c, pair] = small.tile([P, len(units)], F32, name="sums", tag="sums")
                squares[c, pair] = squares_pool.tile([P, len(units), D], F32, name="squares", tag="squares")
            for u in chosen:
                k, e = units[u]
                nc.scalar.activation(
                    out=squares[c, pair][:, u, :],
                    in_=h[c][:, pair * PAIR + e, k, :],
                    func=ACT.Square,
                    accum_out=sums[c, pair][:, u : u + 1],
                )

        def inverse_roots(c, pair):
            inverse[c, pair] = small.tile([P, len(units)], F32, name="inverse", tag="inverse")
            nc.scalar.activation(out=inverse[c, pair][:], in_=sums[c, pair][:], func=ACT.Abs_reciprocal_sqrt)

        def cap_inverse(c, pair):
            rinv[c, pair] = small.tile([P, len(units)], F32, name="rinv", tag="rinv")
            nc.vector.tensor_scalar_min(out=rinv[c, pair][:], in0=inverse[c, pair][:], scalar1=1.0 / EPS)

        def scale(c, pair, split, chosen):
            on_gpsimd, on_scalar, on_vector = split
            for u, (k, e) in enumerate(units):
                rows = h[c][:, pair * PAIR + e, k, :]
                factor = rinv[c, pair][:, u : u + 1]
                if u not in chosen:
                    pass
                elif u < on_gpsimd:
                    nc.gpsimd.tensor_scalar(
                        out=rows, in0=rows, scalar1=factor, scalar2=0.0, op0=ALU.mult, op1=ALU.add
                    )
                elif u < on_gpsimd + on_scalar:
                    nc.scalar.activation(out=rows, in_=rows, func=ACT.Copy, scale=factor)
                else:
                    nc.vector.tensor_scalar_mul(out=rows, in0=rows, scalar1=factor)

        def store_by_units(c, pair, split):
            on_gpsimd, on_scalar, on_vector = split
            ready = [(3 * (u + 1), u) for u in range(on_scalar)] + [(2 * (v + 1), on_scalar + v) for v in range(on_vector)]
            for when, u in sorted(ready):
                k, e = units[u]
                first = c * CHUNK + (pair * PAIR + e) * P
                nc.sync.dma_start(out=out[k, first : first + P, :], in_=h[c][:, pair * PAIR + e, k, :])

        def store(c, pair):
            for i in range(pair * PAIR, (pair + 1) * PAIR):
                first = c * CHUNK + i * P
                nc.sync.dma_start(out=out[:, first : first + P, :].rearrange("k p d -> p k d"), in_=h[c][:, i, :, :])

        w_codes = const.tile([P, PASSES, HEADS * D], U32, name="w_codes", align_bytes=64)
        w_scales = const.tile([P, PASSES, HEADS * D], U8, name="w_scales", align_bytes=64)
        staged = const.tile([P, PASSES, HEADS * D], U8, name="staged", align_bytes=64)
        bias_rows = const.tile([P, HEADS, D], BF16, name="bias_rows")
        ones = const.tile([P, P], BF16, name="ones")
        bias = const.tile([P, HEADS, D], F32, name="bias")
        warm = const.tile([P, 1], F32, name="warm")
        identity = const.tile([P, P], BF16, name="identity")

        words = (W1_words, W2_words, W3_words)
        scale_bytes = (W1_scales, W2_scales, W3_scales)
        biases = (b1, b2, b3)

        def load_words(k):
            nc.sync.dma_start(
                out=w_codes[:, :, k * D : (k + 1) * D].bitcast(I32),
                in_=words[k].rearrange("g p n t -> p g (n t)").bitcast(I32),
            )

        def spread_biases():
            spread12 = psum12.tile([P, 2, D], F32, name="spread12", tag="acc12")
            spread3 = psum3.tile([P, PAIR, D], F32, name="spread3", tag="acc3")
            nc.tensor.matmul(
                out=spread12[:].rearrange("p k d -> p (k d)"),
                lhsT=ones[:],
                rhs=bias_rows[:, 0:2, :].rearrange("p k d -> p (k d)"),
                start=True,
                stop=True,
            )
            nc.tensor.matmul(out=spread3[:, 0, :], lhsT=ones[:], rhs=bias_rows[:, 2, :], start=True, stop=True)
            nc.scalar.copy(out=bias[:, 0:2, :], in_=spread12[:])
            nc.scalar.copy(out=bias[:, 2, :], in_=spread3[:, 0, :])

        nc.vector.memset(w_scales[:].bitcast(I32), 0)
        for k in range(HEADS):
            nc.sync.dma_start(
                out=staged[0:16, :, k * D : (k + 1) * D].bitcast(I32),
                in_=scale_bytes[k].rearrange("g q n -> q g n").bitcast(I32),
            )
        load(nc.scalar, *items[0])
        load(nc.scalar, *items[1])
        load_words(0)
        load(nc.scalar, *items[2])
        load(nc.scalar, *items[3])
        nc.vector.memset(bias_rows[:], 0.0)
        nc.vector.memset(ones[:], 1.0)
        nc.vector.memset(warm[:], 1.0)
        nc.scalar.activation(out=warm[:], in_=warm[:], func=ACT.Abs_reciprocal_sqrt)
        for k in range(HEADS):
            nc.gpsimd.dma_start(out=bias_rows[0:1, k, :], in_=biases[k].rearrange("(o d) -> o d", o=1))
        make_identity(nc, identity[:])
        for quadrant in range(4):
            nc.sync.dma_start(
                out=w_scales[32 * quadrant : 32 * quadrant + 4, :, :].rearrange("p g n -> p (g n)").bitcast(I32),
                in_=staged[4 * quadrant : 4 * quadrant + 4, :, :].rearrange("p g n -> p (g n)").bitcast(I32),
            )
        load_words(1)
        load_words(2)
        for c, g in items[4:]:
            load(nc.sync, c, g)
        regroup(*items[0])
        for i in range(1, REGROUP_LEAD):
            if i == REGROUP_LEAD - 1:
                spread_biases()
            regroup(*items[i])
            quantise(*items[i - 1])

        project12(*steps[0])
        project3(*steps[0])
        interleave(*items[REGROUP_LEAD])

        for q in range(len(steps) + 2):
            for c, pair in at(steps, q):
                add_bias(c, pair)
            for c, pair in at(steps, q - 2):
                on_gpsimd, on_scalar, on_vector = split_of(q - 2)
                late = range(on_gpsimd + on_scalar // 2, on_gpsimd + on_scalar)
                scale(c, pair, split_of(q - 2), [u for u in range(len(units)) if u not in late])
            for c, pair in at(steps, q):
                square_sums(c, pair, range(0, 2))
            for c, pair in at(steps, q - 1):
                inverse_roots(c, pair)
            for c, pair in at(steps, q):
                square_sums(c, pair, range(2, len(units)))
            for c, pair in at(steps, q - 2):
                scale(c, pair, split_of(q - 2), late)
                if (c, pair) == steps[-1]:
                    store_by_units(c, pair, split_of(q - 2))
                else:
                    store(c, pair)
            for c, g in at(items, q + REGROUP_LEAD):
                regroup(c, g)
            gpsimd_regroups_next = q + 1 + REGROUP_LEAD < len(items)
            if gpsimd_regroups_next:
                for c, pair in at(steps, q - 1):
                    cap_inverse(c, pair)
            for c, g in at(items, q + REGROUP_LEAD - 1):
                quantise(c, g)
            for c, pair in at(steps, q + 1):
                project12(c, pair)
                project3(c, pair)
            for c, g in at(items, q + 1 + REGROUP_LEAD):
                interleave(c, g)
            if not gpsimd_regroups_next:
                for c, pair in at(steps, q - 1):
                    cap_inverse(c, pair)
